import numpy as np
import ml_dtypes


def mxq(x, axis, fmt="e4m3"):
    dtype, down = {"e4m3": (ml_dtypes.float8_e4m3fn, 7), "e5m2": (ml_dtypes.float8_e5m2, 14)}[fmt]
    v = np.moveaxis(np.asarray(x, np.float32).astype(ml_dtypes.bfloat16).astype(np.float64), axis, -1)
    blocks = v.reshape(v.shape[:-1] + (-1, 32))
    amax = np.abs(blocks).max(-1, keepdims=True)
    byte = np.maximum(np.where(amax > 0, np.frexp(amax)[1] - 1 + 127, 0) - down, 1)
    scale = np.exp2(byte - 127.0)
    codes = (blocks / scale).astype(np.float32).astype(dtype).astype(np.float64)
    return np.moveaxis((codes * scale).reshape(v.shape), -1, axis)


WIDE = False


def mx_kscale(k):
    if not WIDE:
        return np.ones(k)
    levels = np.array([10, -10, 5, -5, 0])
    if k % 512:
        return np.exp2(np.random.permutation(np.resize(levels, k // 32))).repeat(32)
    a = np.empty((k // 512, 16))
    for p in range(k // 512):
        a[p, :8] = np.random.permutation(np.resize(levels, 8))
        for g in range(8):
            far = levels[np.abs(levels - a[p, g]) >= 10]
            a[p, g + 8] = far[np.random.randint(len(far))]
    return np.exp2(a.ravel()).repeat(32)


BF16 = ml_dtypes.bfloat16


def bf(x):
    return np.asarray(x, np.float32).astype(BF16)


def f64(x):
    return np.asarray(x).astype(np.float64)


B, C, HI, WI, KH, KW, SH, SW, F1, F2, F3 = 2, 16, 70, 70, 8, 8, 2, 2, 1024, 256, 64
K1 = C * KH * KW
HO = (HI - KH) // SH + 1
WO = (WI - KW) // SW + 1
L = HO * WO


def unfold(x):
    cols = [x[:, :, i:i + (HO - 1) * SH + 1:SH, j:j + (WO - 1) * SW + 1:SW] for i in range(KH) for j in range(KW)]
    return np.stack(cols, axis=2).reshape(B, K1, L)


def setup_inputs():
    sc = mx_kscale(K1)[::KH * KW]
    s = np.repeat(sc, KH * KW)
    t = mx_kscale(F1)
    return {"x": bf(np.random.standard_normal((B, C, HI, WI)) * sc[None, :, None, None]),
            "w1": bf(np.random.standard_normal((K1, F1)) / np.sqrt(K1) / s[:, None] * t),
            "b1": bf(np.random.standard_normal(F1) * 0.3 * t),
            "w2": bf(np.random.standard_normal((F1, F2)) * 1.4 / np.sqrt(F1) / t[:, None]),
            "b2": bf(np.random.standard_normal(F2) * 0.3)}


def reference(x, w1, b1, w2, b2):
    p = unfold(f64(x)).transpose(0, 2, 1)
    h1 = np.maximum((mxq(p, 2, "e4m3") @ mxq(f64(w1), 0, "e4m3")) + f64(b1), 0.0)
    return np.maximum((mxq(h1, 2, "e4m3") @ mxq(f64(w2), 0, "e4m3")) + f64(b2), 0.0)

@@ -1,0 +1,278 @@
+from contextlib import ExitStack
+
+import concourse.mybir as mybir
+
+F32 = mybir.dt.float32
+BF16 = mybir.dt.bfloat16
+U32 = mybir.dt.uint32
+U8 = mybir.dt.uint8
+FP8X4 = mybir.dt.float8_e4m3fn_x4
+RELU = mybir.ActivationFunctionType.Relu
+ADD = mybir.AluOpType.add
+MAX = mybir.AluOpType.max
+
+FLOPS = 2 * 2048 * 1024 * 1024 + 2 * 2048 * 1024 * 256
+
+P = 128
+ROWS = 34
+XHALF = 2448
+XLEN = 4686
+ACT_SLABS = {(0, 0): 1, (0, 1): 2, (1, 0): 0, (1, 1): 0}
+W2_SLOT = 8
+R_AGE = 7
+LEAD = 6
+
+
+def tile_mlpconv2d_pa_kernel(tc, x, w1, b1, w2, b2, out):
+    nc = tc.nc
+    with ExitStack() as ctx:
+        keep = ctx.enter_context(tc.tile_pool(name="keep", bufs=1))
+        psum = ctx.enter_context(tc.psum_pool(name="psum", bufs=8))
+
+        xr = [keep.tile([P, ROWS * 140], BF16, name="xr%d" % n, align_bytes=64) for n in range(2)]
+        grp = [keep.tile([P, ROWS * 128], BF16, name="grp%d" % n, align_bytes=64) for n in range(2)]
+        qc = [keep.tile([P, ROWS * 32], U32, name="qc%d" % n, align_bytes=64) for n in range(2)]
+        qs = [keep.tile([P, ROWS * 32], U8, name="qs%d" % n, align_bytes=64) for n in range(2)]
+        w1r = keep.tile([P, 2, 4, 1024], BF16, name="w1r", align_bytes=64)
+        w1g = keep.tile([P, 2, 2, 4, P, 4], BF16, name="w1g", align_bytes=64)
+        w1c = keep.tile([P, 2, 2, 512], U32, name="w1c", align_bytes=64)
+        w1s = keep.tile([P, 2, 2, 512], U8, name="w1s", align_bytes=64)
+        w2r = keep.tile([P, 2, 4, 256], BF16, name="w2r", align_bytes=64)
+        w2g = keep.tile([P, 2, 256, 4], BF16, name="w2g", align_bytes=64)
+        w2c = keep.tile([P, 2, 256], U32, name="w2c", align_bytes=64)
+        w2s = keep.tile([P, 2, 256], U8, name="w2s", align_bytes=64)
+        b1t = keep.tile([P, 8], BF16, name="b1t")
+        b1f = keep.tile([P, 8], F32, name="b1f")
+        b2z = keep.tile([P, 256], BF16, name="b2z")
+        ones = keep.tile([P, P], BF16, name="ones")
+        b2bc = keep.tile([P, 256], F32, name="b2bc")
+        hpl = [keep.tile([P, 8, 512], BF16, name="hpl%d" % t, align_bytes=64) for t in range(4)]
+        hgr = [keep.tile([P, 2, 512, 4], BF16, name="hgr%d" % t, align_bytes=64) for t in range(4)]
+        hc = [keep.tile([P, 2, 512], U32, name="hc%d" % t, align_bytes=64) for t in range(4)]
+        hs = [keep.tile([P, 2, 512], U8, name="hs%d" % t, align_bytes=64) for t in range(4)]
+        res = [keep.tile([P, 4, 256], F32, name="res%d" % t) for t in range(4)]
+
+        xf = x.rearrange("n c h w -> n c (h w)")
+        w1v = w1.rearrange("(c a q t) f -> q a c t f", c=16, a=2, q=8, t=4)
+        outv = out.rearrange("n (h b p) f -> (n h) p b f", h=2, b=4, p=P)
+
+        def load_x(eng, n, q, lo, hi):
+            off = 70 * (q // 2) + 4 * (q % 2)
+            eng.dma_start(out=xr[n][q:P:8, lo:hi], in_=xf[n, :, off + lo : off + hi])
+
+        def load_w1(g, a):
+            cols = slice(512 * g, 512 * g + 512)
+            for q in range(8):
+                nc.sync.dma_start(out=w1r[q:P:8, a, :, cols], in_=w1v[q, a, :, :, cols])
+
+        ctx.enter_context(tc.manual_schedule())
+        nc.vector.memset(b2z[:], 0.0)
+        nc.vector.memset(ones[:], 1.0)
+        nc.gpsimd.dma_start(
+            out=b1t[:].rearrange("p (g t) -> p g t", g=2), in_=b1.rearrange("(g p t) -> p g t", g=2, t=4)
+        )
+        nc.gpsimd.dma_start(out=b2z[0:1, :], in_=b2.rearrange("(o n) -> o n", o=1))
+        for q in range(8):
+            load_x(nc.scalar if q < 4 else nc.sync, 0, q, 0, XHALF)
+        load_w1(0, 0)
+        load_w1(0, 1)
+        for q in range(8):
+            load_x(nc.sync, 0, q, XHALF, XLEN)
+        load_w1(1, 0)
+        load_w1(1, 1)
+        nc.sync.dma_start(out=w2r[:], in_=w2.rearrange("(g p t) n -> p g t n", g=2, t=4))
+        for q in range(8):
+            load_x(nc.sync, 1, q, 0, XLEN)
+
+        def copy_p(t):
+            n, r0, r1 = t // 2, 18 * (t % 2), 18 + 16 * (t % 2)
+            x32 = xr[n][:].bitcast(F32).rearrange("p (u w) -> p u w", w=70)
+            g32 = grp[n][:].bitcast(F32).rearrange("p (u par w) -> p u par w", par=2, w=32)
+            for par in range(2):
+                nc.vector.tensor_copy(out=g32[:, r0:r1, par, :], in_=x32[:, r0:r1, par : par + 32])
+
+        def quant_p(t):
+            n = t // 2
+            for c0, c1 in ((0, 512), (512, 576)) if t % 2 == 0 else ((576, 1088),):
+                nc.vector.quantize_mx(
+                    out=qc[n][:, c0:c1].bitcast(FP8X4), scales=qs[n][:, c0:c1], in_=grp[n][:, 4 * c0 : 4 * c1]
+                )
+
+        def regroup(eng_copy, dst, src):
+            eng_copy(
+                out=dst.rearrange("p (c i) t -> p c t i", i=4),
+                in_=src.rearrange("p t (c i) -> p c t i", i=4),
+            )
+
+        def regroup_w1(g, a):
+            src = w1r[:, a, :, 512 * g : 512 * g + 512].rearrange("p t (m tp) -> p tp m t", tp=4)
+            nv = 4 - ACT_SLABS[(g, a)]
+            nc.vector.tensor_copy(out=w1g[:, g, a, 0:nv, :, :], in_=src[:, 0:nv, :, :])
+            for tp in range(nv, 4):
+                nc.scalar.copy(out=w1g[:, g, a, tp, :, :], in_=src[:, tp, :, :])
+
+        def quant_w1(g, a):
+            nc.vector.quantize_mx(
+                out=w1c[:, g, a, :].bitcast(FP8X4),
+                scales=w1s[:, g, a, :],
+                in_=w1g[:, g, a, :, :, :].rearrange("p tp m t -> p (tp m t)"),
+            )
+
+        units = [(t, 4 * g + k) for g in range(2) for t in range(2) for k in range(4)]
+        units += [(t, ft) for t in (2, 3) for ft in range(8)]
+        banks = {}
+
+        def l1_pass(u, a):
+            t, ft = units[u]
+            if a == 0:
+                banks[u] = psum.tile([P, 512], F32, name="l1_%d" % u, tag="bank")
+            g, c0 = ft // 4, P * (ft % 4)
+            r0 = 512 * (t % 2) + 64 * a
+            nc.tensor.matmul_mx(
+                out=banks[u][:],
+                lhsT=w1c[:, g, a, c0 : c0 + P].bitcast(FP8X4),
+                lhsT_scale=w1s[:, g, a, c0 : c0 + P],
+                rhs=qc[t // 2][:, r0 : r0 + 512].bitcast(FP8X4),
+                rhs_scale=qs[t // 2][:, r0 : r0 + 512],
+                start=(a == 0),
+                stop=(a == 1),
+            )
+
+        def l1(u):
+            l1_pass(u, 0)
+            l1_pass(u, 1)
+
+        def evac(u):
+            t, ft = units[u]
+            nc.scalar.activation(
+                out=hpl[t][:, ft, :].rearrange("p (u vh par) -> p u vh par", u=16, par=2),
+                in_=banks[u][:].rearrange("p (u par vh) -> p u vh par", u=16, par=2),
+                func=RELU,
+                bias=b1f[:, ft : ft + 1],
+                scale=1.0,
+            )
+
+        def regroup_h(t, g, c0=0, c1=512, eng_copy=None):
+            regroup(eng_copy or nc.vector.tensor_copy, hgr[t][:, g, c0:c1, :], hpl[t][:, 4 * g : 4 * g + 4, c0:c1])
+
+        def quant_h(t, g, c0=0, c1=512):
+            nc.vector.quantize_mx(
+                out=hc[t][:, g, c0:c1].bitcast(FP8X4),
+                scales=hs[t][:, g, c0:c1],
+                in_=hgr[t][:, g, c0:c1, :].rearrange("p c t -> p (c t)"),
+            )
+
+        accs = {}
+
+        def l2(t, k):
+            acc = psum.tile([P, 2, 256], F32, name="acc%d_%d" % (t, k), tag="bank")
+            accs[(t, k)] = acc
+            for s in range(2):
+                c0 = P * (2 * k + s)
+                for g in range(2):
+                    nc.tensor.matmul_mx(
+                        out=acc[:, s, :],
+                        lhsT=hc[t][:, g, c0 : c0 + P].bitcast(FP8X4),
+                        lhsT_scale=hs[t][:, g, c0 : c0 + P],
+                        rhs=w2c[:, g, :].bitcast(FP8X4),
+                        rhs_scale=w2s[:, g, :],
+                        start=(g == 0),
+                        stop=(g == 1),
+                    )
+
+        def add_b2(t, k):
+            nc.vector.tensor_tensor(
+                out=res[t][:, 2 * k : 2 * k + 2, :],
+                in0=accs[(t, k)][:],
+                in1=b2bc[:].unsqueeze(1).to_broadcast([P, 2, 256]),
+                op=ADD,
+            )
+
+        def relu_store(t, k, on_vector=False, halves=False):
+            r = res[t][:, 2 * k : 2 * k + 2, :]
+            if on_vector:
+                nc.vector.tensor_scalar(out=r, in0=r, scalar1=0.0, scalar2=None, op0=MAX)
+            else:
+                nc.scalar.activation(out=r, in_=r, func=RELU)
+            if halves or k == 1:
+                b0 = 2 * k if halves else 0
+                nc.sync.dma_start(out=outv[t][:, b0 : 2 * k + 2, :], in_=res[t][:, b0 : 2 * k + 2, :])
+
+        def half_done(s, age):
+            if 0 <= s - age < 31 and units[s - age][1] % 4 == 3:
+                return units[s - age][0], units[s - age][1] // 4
+            return None, None
+
+        copy_p(0)
+        nc.vector.tensor_copy(out=b1f[:], in_=b1t[:])
+        regroup_w1(0, 0)
+        quant_p(0)
+        quant_w1(0, 0)
+        for u in range(4):
+            l1_pass(u, 0)
+        regroup_w1(0, 1)
+        copy_p(1)
+        quant_w1(0, 1)
+        for u in range(4):
+            l1_pass(u, 1)
+        quant_p(1)
+        l1(4)
+        l1(5)
+        b2ps = psum.tile([P, 512], F32, name="b2ps", tag="bank")
+        nc.tensor.matmul(out=b2ps[:, 0:256], lhsT=ones[:], rhs=b2z[:], start=True, stop=True)
+        prep = {
+            0: [lambda: regroup_w1(1, 0)],
+            1: [lambda: regroup_w1(1, 1), lambda: quant_w1(1, 0)],
+            2: [lambda: quant_w1(1, 1)],
+            8: [lambda: copy_p(2)],
+            9: [lambda: quant_p(2)],
+            16: [lambda: copy_p(3)],
+            17: [lambda: quant_p(3)],
+        }
+        for s in range(32):
+            evac(s)
+            if s == 5:
+                nc.vector.tensor_copy(out=b2bc[:], in_=b2ps[:, 0:256])
+            for f in prep.get(s, []):
+                f()
+            if s + LEAD < 32:
+                l1(s + LEAD)
+            t, g = half_done(s, 0)
+            if g is not None:
+                regroup_h(t, g, 0, 256)
+                regroup_h(t, g, 256, 512)
+            if s == W2_SLOT:
+                for gg in range(2):
+                    regroup(nc.scalar.copy, w2g[:, gg, :, :], w2r[:, gg, :, :])
+            if s == W2_SLOT + 2:
+                nc.vector.quantize_mx(
+                    out=w2c[:].rearrange("p g n -> p (g n)").bitcast(FP8X4),
+                    scales=w2s[:].rearrange("p g n -> p (g n)"),
+                    in_=w2g[:].rearrange("p g n t -> p (g n t)"),
+                )
+            t, g = half_done(s, 1)
+            if g is not None:
+                quant_h(t, g, 0, 256)
+                quant_h(t, g, 256, 512)
+                if g == 1:
+                    l2(t, 0)
+                    l2(t, 1)
+            for k in range(2):
+                t, g = half_done(s, 2 + k)
+                if g == 1:
+                    add_b2(t, k)
+                t, g = half_done(s, R_AGE + k)
+                if g == 1:
+                    relu_store(t, k)
+
+        for c0 in (0, 128):
+            regroup_h(3, 1, c0, c0 + 128)
+            regroup_h(3, 1, c0 + 256, c0 + 384, nc.scalar.copy)
+        for k in range(2):
+            for c0 in (256 * k, 256 * k + 128):
+                quant_h(3, 1, c0, c0 + 128)
+            l2(3, k)
+        add_b2(3, 0)
+        relu_store(3, 0, halves=True)
+        add_b2(3, 1)
+        relu_store(3, 1, on_vector=True, halves=True)

@@ -17,7 +17,7 @@ P = 128
 ROWS = 34
 XHALF = 2448
 XLEN = 4686
-ACT_SLABS = {(0, 0): 1, (0, 1): 2, (1, 0): 0, (1, 1): 0}
+ACT_SLABS = {(0, 0): 2, (1, 0): 2, (0, 1): 1, (1, 1): 2}
 W2_SLOT = 8
 R_AGE = 7
 LEAD = 6
@@ -46,6 +46,7 @@ def tile_mlpconv2d_pa_kernel(tc, x, w1, b1, w2, b2, out):
         b2z = keep.tile([P, 256], BF16, name="b2z")
         ones = keep.tile([P, P], BF16, name="ones")
         b2bc = keep.tile([P, 256], F32, name="b2bc")
+        warm = keep.tile([P, 1], BF16, name="warm")
         hpl = [keep.tile([P, 8, 512], BF16, name="hpl%d" % t, align_bytes=64) for t in range(4)]
         hgr = [keep.tile([P, 2, 512, 4], BF16, name="hgr%d" % t, align_bytes=64) for t in range(4)]
         hc = [keep.tile([P, 2, 512], U32, name="hc%d" % t, align_bytes=64) for t in range(4)]
@@ -60,26 +61,25 @@ def tile_mlpconv2d_pa_kernel(tc, x, w1, b1, w2, b2, out):
             off = 70 * (q // 2) + 4 * (q % 2)
             eng.dma_start(out=xr[n][q:P:8, lo:hi], in_=xf[n, :, off + lo : off + hi])
 
-        def load_w1(g, a):
-            cols = slice(512 * g, 512 * g + 512)
+        def load_w1(a, first_queue):
             for q in range(8):
-                nc.sync.dma_start(out=w1r[q:P:8, a, :, cols], in_=w1v[q, a, :, :, cols])
+                eng = first_queue if q < 4 else nc.sync
+                eng.dma_start(out=w1r[q:P:8, a, :, :], in_=w1v[q, a, :, :, :])
 
         ctx.enter_context(tc.manual_schedule())
         nc.vector.memset(b2z[:], 0.0)
         nc.vector.memset(ones[:], 1.0)
+        nc.gpsimd.dma_start(out=b2z[0:1, :], in_=b2.rearrange("(o n) -> o n", o=1))
         nc.gpsimd.dma_start(
             out=b1t[:].rearrange("p (g t) -> p g t", g=2), in_=b1.rearrange("(g p t) -> p g t", g=2, t=4)
         )
-        nc.gpsimd.dma_start(out=b2z[0:1, :], in_=b2.rearrange("(o n) -> o n", o=1))
+        load_w1(0, nc.scalar)
+        nc.scalar.activation(out=warm[:], in_=ones[:, 0:1], func=RELU)
         for q in range(8):
             load_x(nc.scalar if q < 4 else nc.sync, 0, q, 0, XHALF)
-        load_w1(0, 0)
-        load_w1(0, 1)
+        load_w1(1, nc.sync)
         for q in range(8):
             load_x(nc.sync, 0, q, XHALF, XLEN)
-        load_w1(1, 0)
-        load_w1(1, 1)
         nc.sync.dma_start(out=w2r[:], in_=w2.rearrange("(g p t) n -> p g t n", g=2, t=4))
         for q in range(8):
             load_x(nc.sync, 1, q, 0, XLEN)
@@ -203,27 +203,28 @@ def tile_mlpconv2d_pa_kernel(tc, x, w1, b1, w2, b2, out):
                 return units[s - age][0], units[s - age][1] // 4
             return None, None
 
-        copy_p(0)
-        nc.vector.tensor_copy(out=b1f[:], in_=b1t[:])
         regroup_w1(0, 0)
-        quant_p(0)
+        regroup_w1(1, 0)
         quant_w1(0, 0)
+        copy_p(0)
+        quant_w1(1, 0)
+        quant_p(0)
+        nc.vector.tensor_copy(out=b1f[:], in_=b1t[:])
         for u in range(4):
             l1_pass(u, 0)
         regroup_w1(0, 1)
-        copy_p(1)
+        regroup_w1(1, 1)
         quant_w1(0, 1)
         for u in range(4):
             l1_pass(u, 1)
+        copy_p(1)
+        quant_w1(1, 1)
         quant_p(1)
         l1(4)
         l1(5)
         b2ps = psum.tile([P, 512], F32, name="b2ps", tag="bank")
         nc.tensor.matmul(out=b2ps[:, 0:256], lhsT=ones[:], rhs=b2z[:], start=True, stop=True)
         prep = {
-            0: [lambda: regroup_w1(1, 0)],
-            1: [lambda: regroup_w1(1, 1), lambda: quant_w1(1, 0)],
-            2: [lambda: quant_w1(1, 1)],
             8: [lambda: copy_p(2)],
             9: [lambda: quant_p(2)],
             16: [lambda: copy_p(3)],

@@ -51,11 +51,12 @@ def tile_mlpconv2d_pa_kernel(tc, x, w1, b1, w2, b2, out):
         hgr = [keep.tile([P, 2, 512, 4], BF16, name="hgr%d" % t, align_bytes=64) for t in range(4)]
         hc = [keep.tile([P, 2, 512], U32, name="hc%d" % t, align_bytes=64) for t in range(4)]
         hs = [keep.tile([P, 2, 512], U8, name="hs%d" % t, align_bytes=64) for t in range(4)]
-        res = [keep.tile([P, 4, 256], F32, name="res%d" % t) for t in range(4)]
+        res = [keep.tile([P, 2, 2, 256], F32, name="res%d" % t) for t in range(4)]
 
         xf = x.rearrange("n c h w -> n c (h w)")
         w1v = w1.rearrange("(c a q t) f -> q a c t f", c=16, a=2, q=8, t=4)
-        outv = out.rearrange("n (h b p) f -> (n h) p b f", h=2, b=4, p=P)
+        outv = out.rearrange("n (h uh m par) f -> (n h) par m uh f", h=2, uh=2, m=P, par=2)
+        outw = out.rearrange("n (h uh m par) f -> (n h) m uh (par f)", h=2, uh=2, m=P, par=2)
 
         def load_x(eng, n, q, lo, hi):
             off = 70 * (q // 2) + 4 * (q % 2)
@@ -145,8 +146,8 @@ def tile_mlpconv2d_pa_kernel(tc, x, w1, b1, w2, b2, out):
         def evac(u):
             t, ft = units[u]
             nc.scalar.activation(
-                out=hpl[t][:, ft, :].rearrange("p (u vh par) -> p u vh par", u=16, par=2),
-                in_=banks[u][:].rearrange("p (u par vh) -> p u vh par", u=16, par=2),
+                out=hpl[t][:, ft, :].rearrange("p (par u vh) -> p par u vh", u=16, par=2),
+                in_=banks[u][:].rearrange("p (u par vh) -> p par u vh", u=16, par=2),
                 func=RELU,
                 bias=b1f[:, ft : ft + 1],
                 scale=1.0,
@@ -182,21 +183,22 @@ def tile_mlpconv2d_pa_kernel(tc, x, w1, b1, w2, b2, out):
 
         def add_b2(t, k):
             nc.vector.tensor_tensor(
-                out=res[t][:, 2 * k : 2 * k + 2, :],
+                out=res[t][:, :, k, :],
                 in0=accs[(t, k)][:],
                 in1=b2bc[:].unsqueeze(1).to_broadcast([P, 2, 256]),
                 op=ADD,
             )
 
         def relu_store(t, k, on_vector=False, halves=False):
-            r = res[t][:, 2 * k : 2 * k + 2, :]
+            r = res[t][:, :, k, :]
             if on_vector:
                 nc.vector.tensor_scalar(out=r, in0=r, scalar1=0.0, scalar2=None, op0=MAX)
             else:
                 nc.scalar.activation(out=r, in_=r, func=RELU)
-            if halves or k == 1:
-                b0 = 2 * k if halves else 0
-                nc.sync.dma_start(out=outv[t][:, b0 : 2 * k + 2, :], in_=res[t][:, b0 : 2 * k + 2, :])
+            if halves:
+                nc.sync.dma_start(out=outv[t, k], in_=r)
+            elif k == 1:
+                nc.sync.dma_start(out=outw[t], in_=res[t][:].rearrange("p uh par f -> p uh (par f)"))
 
         def half_done(s, age):
             if 0 <= s - age < 31 and units[s - age][1] % 4 == 3:

@@ -29,11 +29,14 @@ def tile_mlpconv2d_pa_kernel(tc, x, w1, b1, w2, b2, out):
         keep = ctx.enter_context(tc.tile_pool(name="keep", bufs=1))
         psum = ctx.enter_context(tc.psum_pool(name="psum", bufs=8))
 
-        xr = [keep.tile([P, ROWS * 140], BF16, name="xr%d" % n, align_bytes=64) for n in range(2)]
+        xa = keep.tile([P, 18 * 140], BF16, name="xa", align_bytes=64)
+        xb = keep.tile([P, 16 * 140], BF16, name="xb", align_bytes=64)
+        x1 = keep.tile([P, ROWS * 140], BF16, name="x1", align_bytes=64)
+        xsrc = ((xa, 0), (xb, 0), (x1, 0), (x1, 18))
         grp = [keep.tile([P, ROWS * 128], BF16, name="grp%d" % n, align_bytes=64) for n in range(2)]
         qc = [keep.tile([P, ROWS * 32], U32, name="qc%d" % n, align_bytes=64) for n in range(2)]
         qs = [keep.tile([P, ROWS * 32], U8, name="qs%d" % n, align_bytes=64) for n in range(2)]
-        w1r = keep.tile([P, 2, 4, 1024], BF16, name="w1r", align_bytes=64)
+        w1r = [keep.tile([P, 4, 1024], BF16, name="w1r%d" % a, align_bytes=64) for a in range(2)]
         w1g = keep.tile([P, 2, 2, 4, P, 4], BF16, name="w1g", align_bytes=64)
         w1c = keep.tile([P, 2, 2, 512], U32, name="w1c", align_bytes=64)
         w1s = keep.tile([P, 2, 2, 512], U8, name="w1s", align_bytes=64)
@@ -58,14 +61,14 @@ def tile_mlpconv2d_pa_kernel(tc, x, w1, b1, w2, b2, out):
         outv = out.rearrange("n (h uh m par) f -> (n h) par m uh f", h=2, uh=2, m=P, par=2)
         outw = out.rearrange("n (h uh m par) f -> (n h) m uh (par f)", h=2, uh=2, m=P, par=2)
 
-        def load_x(eng, n, q, lo, hi):
+        def load_x(eng, dst, n, q, lo, hi):
             off = 70 * (q // 2) + 4 * (q % 2)
-            eng.dma_start(out=xr[n][q:P:8, lo:hi], in_=xf[n, :, off + lo : off + hi])
+            eng.dma_start(out=dst[q:P:8, 0 : hi - lo], in_=xf[n, :, off + lo : off + hi])
 
         def load_w1(a, first_queue):
             for q in range(8):
                 eng = first_queue if q < 4 else nc.sync
-                eng.dma_start(out=w1r[q:P:8, a, :, :], in_=w1v[q, a, :, :, :])
+                eng.dma_start(out=w1r[a][q:P:8, :, :], in_=w1v[q, a, :, :, :])
 
         ctx.enter_context(tc.manual_schedule())
         nc.vector.memset(b2z[:], 0.0)
@@ -77,20 +80,21 @@ def tile_mlpconv2d_pa_kernel(tc, x, w1, b1, w2, b2, out):
         load_w1(0, nc.scalar)
         nc.scalar.activation(out=warm[:], in_=ones[:, 0:1], func=RELU)
         for q in range(8):
-            load_x(nc.scalar if q < 4 else nc.sync, 0, q, 0, XHALF)
+            load_x(nc.scalar if q < 4 else nc.sync, xa, 0, q, 0, XHALF)
         load_w1(1, nc.sync)
         for q in range(8):
-            load_x(nc.sync, 0, q, XHALF, XLEN)
+            load_x(nc.sync, xb, 0, q, 18 * 140, XLEN)
         nc.sync.dma_start(out=w2r[:], in_=w2.rearrange("(g p t) n -> p g t n", g=2, t=4))
         for q in range(8):
-            load_x(nc.sync, 1, q, 0, XLEN)
+            load_x(nc.sync, x1, 1, q, 0, XLEN)
 
         def copy_p(t):
             n, r0, r1 = t // 2, 18 * (t % 2), 18 + 16 * (t % 2)
-            x32 = xr[n][:].bitcast(F32).rearrange("p (u w) -> p u w", w=70)
+            src, s0 = xsrc[t]
+            x32 = src[:].bitcast(F32).rearrange("p (u w) -> p u w", w=70)
             g32 = grp[n][:].bitcast(F32).rearrange("p (u par w) -> p u par w", par=2, w=32)
             for par in range(2):
-                nc.vector.tensor_copy(out=g32[:, r0:r1, par, :], in_=x32[:, r0:r1, par : par + 32])
+                nc.vector.tensor_copy(out=g32[:, r0:r1, par, :], in_=x32[:, s0 : s0 + r1 - r0, par : par + 32])
 
         def quant_p(t):
             n = t // 2
@@ -106,7 +110,7 @@ def tile_mlpconv2d_pa_kernel(tc, x, w1, b1, w2, b2, out):
             )
 
         def regroup_w1(g, a):
-            src = w1r[:, a, :, 512 * g : 512 * g + 512].rearrange("p t (m tp) -> p tp m t", tp=4)
+            src = w1r[a][:, :, 512 * g : 512 * g + 512].rearrange("p t (m tp) -> p tp m t", tp=4)
             nv = 4 - ACT_SLABS[(g, a)]
             nc.vector.tensor_copy(out=w1g[:, g, a, 0:nv, :, :], in_=src[:, 0:nv, :, :])
             for tp in range(nv, 4):
@@ -180,6 +184,31 @@ def tile_mlpconv2d_pa_kernel(tc, x, w1, b1, w2, b2, out):
                         start=(g == 0),
                         stop=(g == 1),
                     )
+
+        last = {}
+
+        def l2_block(b, g):
+            if g == 0:
+                last[b] = psum.tile([P, 512], F32, name="last%d" % b, tag="bank")
+            nc.tensor.matmul_mx(
+                out=last[b][:, 0:256],
+                lhsT=hc[3][:, g, P * b : P * b + P].bitcast(FP8X4),
+                lhsT_scale=hs[3][:, g, P * b : P * b + P],
+                rhs=w2c[:, g, :].bitcast(FP8X4),
+                rhs_scale=w2s[:, g, :],
+                start=(g == 0),
+                stop=(g == 1),
+            )
+
+        def add_block(b):
+            nc.vector.tensor_tensor(out=res[3][:, b % 2, b // 2, :], in0=last[b][:, 0:256], in1=b2bc[:], op=ADD)
+
+        def relu_block(b, on_vector=False):
+            r = res[3][:, b % 2, b // 2, :]
+            if on_vector:
+                nc.vector.tensor_scalar(out=r, in0=r, scalar1=0.0, scalar2=None, op0=MAX)
+            else:
+                nc.scalar.activation(out=r, in_=r, func=RELU)
 
         def add_b2(t, k):
             nc.vector.tensor_tensor(
@@ -260,22 +289,31 @@ def tile_mlpconv2d_pa_kernel(tc, x, w1, b1, w2, b2, out):
                 if g == 1:
                     l2(t, 0)
                     l2(t, 1)
+                elif t == 3:
+                    for b in range(4):
+                        l2_block(b, 0)
             for k in range(2):
-                t, g = half_done(s, 2 + k)
+                t, g = half_done(s, 3 + k)
                 if g == 1:
                     add_b2(t, k)
                 t, g = half_done(s, R_AGE + k)
                 if g == 1:
                     relu_store(t, k)
 
-        for c0 in (0, 128):
-            regroup_h(3, 1, c0, c0 + 128)
-            regroup_h(3, 1, c0 + 256, c0 + 384, nc.scalar.copy)
-        for k in range(2):
-            for c0 in (256 * k, 256 * k + 128):
-                quant_h(3, 1, c0, c0 + 128)
-            l2(3, k)
-        add_b2(3, 0)
-        relu_store(3, 0, halves=True)
-        add_b2(3, 1)
-        relu_store(3, 1, on_vector=True, halves=True)
+        for b in range(4):
+            regroup_h(3, 1, P * b, P * b + P, nc.vector.tensor_copy if b % 2 == 0 else nc.scalar.copy)
+        for b in range(3):
+            quant_h(3, 1, P * b, P * b + P)
+            l2_block(b, 1)
+        add_block(0)
+        quant_h(3, 1, 3 * P, 4 * P)
+        l2_block(3, 1)
+        add_block(1)
+        relu_block(0)
+        relu_block(1)
+        nc.sync.dma_start(out=outv[3, 0], in_=res[3][:, :, 0, :])
+        add_block(2)
+        add_block(3)
+        relu_block(2)
+        relu_block(3, on_vector=True)
+        nc.sync.dma_start(out=outv[3, 1], in_=res[3][:, :, 1, :])

@@ -17,7 +17,7 @@ P = 128
 ROWS = 34
 XHALF = 2448
 XLEN = 4686
-ACT_SLABS = {(0, 0): 2, (1, 0): 2, (0, 1): 1, (1, 1): 2}
+ACT_SLABS = {(0, 0): 2, (0, 1): 2, (1, 0): 2, (1, 1): 0}
 W2_SLOT = 8
 R_AGE = 7
 LEAD = 6
@@ -36,7 +36,9 @@ def tile_mlpconv2d_pa_kernel(tc, x, w1, b1, w2, b2, out):
         grp = [keep.tile([P, ROWS * 128], BF16, name="grp%d" % n, align_bytes=64) for n in range(2)]
         qc = [keep.tile([P, ROWS * 32], U32, name="qc%d" % n, align_bytes=64) for n in range(2)]
         qs = [keep.tile([P, ROWS * 32], U8, name="qs%d" % n, align_bytes=64) for n in range(2)]
-        w1r = [keep.tile([P, 4, 1024], BF16, name="w1r%d" % a, align_bytes=64) for a in range(2)]
+        w1r = [
+            [keep.tile([P, 4, 512], BF16, name="w1r%d%d" % (g, a), align_bytes=64) for a in range(2)] for g in range(2)
+        ]
         w1g = keep.tile([P, 2, 2, 4, P, 4], BF16, name="w1g", align_bytes=64)
         w1c = keep.tile([P, 2, 2, 512], U32, name="w1c", align_bytes=64)
         w1s = keep.tile([P, 2, 2, 512], U8, name="w1s", align_bytes=64)
@@ -65,26 +67,28 @@ def tile_mlpconv2d_pa_kernel(tc, x, w1, b1, w2, b2, out):
             off = 70 * (q // 2) + 4 * (q % 2)
             eng.dma_start(out=dst[q:P:8, 0 : hi - lo], in_=xf[n, :, off + lo : off + hi])
 
-        def load_w1(a, first_queue):
+        def load_w1(g, a, first_queue):
             for q in range(8):
                 eng = first_queue if q < 4 else nc.sync
-                eng.dma_start(out=w1r[a][q:P:8, :, :], in_=w1v[q, a, :, :, :])
+                eng.dma_start(out=w1r[g][a][q:P:8, :, :], in_=w1v[q, a, :, :, 512 * g : 512 * g + 512])
 
         ctx.enter_context(tc.manual_schedule())
         nc.vector.memset(b2z[:], 0.0)
         nc.vector.memset(ones[:], 1.0)
+        nc.gpsimd.dma_start(out=w2r[:], in_=w2.rearrange("(g p t) n -> p g t n", g=2, t=4))
         nc.gpsimd.dma_start(out=b2z[0:1, :], in_=b2.rearrange("(o n) -> o n", o=1))
         nc.gpsimd.dma_start(
             out=b1t[:].rearrange("p (g t) -> p g t", g=2), in_=b1.rearrange("(g p t) -> p g t", g=2, t=4)
         )
-        load_w1(0, nc.scalar)
-        nc.scalar.activation(out=warm[:], in_=ones[:, 0:1], func=RELU)
         for q in range(8):
             load_x(nc.scalar if q < 4 else nc.sync, xa, 0, q, 0, XHALF)
-        load_w1(1, nc.sync)
+        nc.scalar.activation(out=warm[:], in_=ones[:, 0:1], func=RELU)
+        load_w1(0, 0, nc.scalar)
+        load_w1(0, 1, nc.sync)
         for q in range(8):
             load_x(nc.sync, xb, 0, q, 18 * 140, XLEN)
-        nc.sync.dma_start(out=w2r[:], in_=w2.rearrange("(g p t) n -> p g t n", g=2, t=4))
+        load_w1(1, 0, nc.sync)
+        load_w1(1, 1, nc.sync)
         for q in range(8):
             load_x(nc.sync, x1, 1, q, 0, XLEN)
 
@@ -110,7 +114,7 @@ def tile_mlpconv2d_pa_kernel(tc, x, w1, b1, w2, b2, out):
             )
 
         def regroup_w1(g, a):
-            src = w1r[a][:, :, 512 * g : 512 * g + 512].rearrange("p t (m tp) -> p tp m t", tp=4)
+            src = w1r[g][a][:].rearrange("p t (m tp) -> p tp m t", tp=4)
             nv = 4 - ACT_SLABS[(g, a)]
             nc.vector.tensor_copy(out=w1g[:, g, a, 0:nv, :, :], in_=src[:, 0:nv, :, :])
             for tp in range(nv, 4):
@@ -234,28 +238,29 @@ def tile_mlpconv2d_pa_kernel(tc, x, w1, b1, w2, b2, out):
                 return units[s - age][0], units[s - age][1] // 4
             return None, None
 
-        regroup_w1(0, 0)
-        regroup_w1(1, 0)
-        quant_w1(0, 0)
         copy_p(0)
-        quant_w1(1, 0)
+        regroup_w1(0, 0)
         quant_p(0)
-        nc.vector.tensor_copy(out=b1f[:], in_=b1t[:])
+        quant_w1(0, 0)
         for u in range(4):
             l1_pass(u, 0)
         regroup_w1(0, 1)
-        regroup_w1(1, 1)
+        for gg in range(2):
+            regroup(nc.scalar.copy, w2g[:, gg, :, :], w2r[:, gg, :, :])
+        nc.vector.tensor_copy(out=b1f[:], in_=b1t[:])
         quant_w1(0, 1)
         for u in range(4):
             l1_pass(u, 1)
         copy_p(1)
-        quant_w1(1, 1)
         quant_p(1)
         l1(4)
         l1(5)
         b2ps = psum.tile([P, 512], F32, name="b2ps", tag="bank")
         nc.tensor.matmul(out=b2ps[:, 0:256], lhsT=ones[:], rhs=b2z[:], start=True, stop=True)
         prep = {
+            0: [lambda: regroup_w1(1, 0)],
+            1: [lambda: regroup_w1(1, 1), lambda: quant_w1(1, 0)],
+            2: [lambda: quant_w1(1, 1)],
             8: [lambda: copy_p(2)],
             9: [lambda: quant_p(2)],
             16: [lambda: copy_p(3)],
@@ -273,9 +278,6 @@ def tile_mlpconv2d_pa_kernel(tc, x, w1, b1, w2, b2, out):
             if g is not None:
                 regroup_h(t, g, 0, 256)
                 regroup_h(t, g, 256, 512)
-            if s == W2_SLOT:
-                for gg in range(2):
-                    regroup(nc.scalar.copy, w2g[:, gg, :, :], w2r[:, gg, :, :])
             if s == W2_SLOT + 2:
                 nc.vector.quantize_mx(
                     out=w2c[:].rearrange("p g n -> p (g n)").bitcast(FP8X4),

@@ -20,6 +20,7 @@ XLEN = 4686
 ACT_SLABS = {(0, 0): 2, (0, 1): 2, (1, 0): 2, (1, 1): 0}
 W2_SLOT = 8
 R_AGE = 7
+QORDER = (0, 4, 1, 5, 2, 6, 3, 7)
 LEAD = 6
 
 
@@ -68,7 +69,7 @@ def tile_mlpconv2d_pa_kernel(tc, x, w1, b1, w2, b2, out):
             eng.dma_start(out=dst[q:P:8, 0 : hi - lo], in_=xf[n, :, off + lo : off + hi])
 
         def load_w1(g, a, first_queue):
-            for q in range(8):
+            for q in QORDER:
                 eng = first_queue if q < 4 else nc.sync
                 eng.dma_start(out=w1r[g][a][q:P:8, :, :], in_=w1v[q, a, :, :, 512 * g : 512 * g + 512])
 
@@ -80,16 +81,16 @@ def tile_mlpconv2d_pa_kernel(tc, x, w1, b1, w2, b2, out):
         nc.gpsimd.dma_start(
             out=b1t[:].rearrange("p (g t) -> p g t", g=2), in_=b1.rearrange("(g p t) -> p g t", g=2, t=4)
         )
-        for q in range(8):
+        for q in QORDER:
             load_x(nc.scalar if q < 4 else nc.sync, xa, 0, q, 0, XHALF)
         nc.scalar.activation(out=warm[:], in_=ones[:, 0:1], func=RELU)
         load_w1(0, 0, nc.scalar)
         load_w1(0, 1, nc.sync)
-        for q in range(8):
+        for q in QORDER:
             load_x(nc.sync, xb, 0, q, 18 * 140, XLEN)
         load_w1(1, 0, nc.sync)
         load_w1(1, 1, nc.sync)
-        for q in range(8):
+        for q in QORDER:
             load_x(nc.sync, x1, 1, q, 0, XLEN)
 
         def copy_p(t):

@@ -76,7 +76,6 @@ def tile_mlpconv2d_pa_kernel(tc, x, w1, b1, w2, b2, out):
         ctx.enter_context(tc.manual_schedule())
         nc.vector.memset(b2z[:], 0.0)
         nc.vector.memset(ones[:], 1.0)
-        nc.gpsimd.dma_start(out=w2r[:], in_=w2.rearrange("(g p t) n -> p g t n", g=2, t=4))
         nc.gpsimd.dma_start(out=b2z[0:1, :], in_=b2.rearrange("(o n) -> o n", o=1))
         nc.gpsimd.dma_start(
             out=b1t[:].rearrange("p (g t) -> p g t", g=2), in_=b1.rearrange("(g p t) -> p g t", g=2, t=4)
@@ -86,6 +85,7 @@ def tile_mlpconv2d_pa_kernel(tc, x, w1, b1, w2, b2, out):
         nc.scalar.activation(out=warm[:], in_=ones[:, 0:1], func=RELU)
         load_w1(0, 0, nc.scalar)
         load_w1(0, 1, nc.sync)
+        nc.sync.dma_start(out=w2r[:], in_=w2.rearrange("(g p t) n -> p g t n", g=2, t=4))
         for q in QORDER:
             load_x(nc.sync, xb, 0, q, 18 * 140, XLEN)
         load_w1(1, 0, nc.sync)
@@ -240,18 +240,20 @@ def tile_mlpconv2d_pa_kernel(tc, x, w1, b1, w2, b2, out):
             return None, None
 
         copy_p(0)
-        regroup_w1(0, 0)
         quant_p(0)
+        regroup_w1(0, 0)
         quant_w1(0, 0)
-        for u in range(4):
+        for u in range(2):
             l1_pass(u, 0)
         regroup_w1(0, 1)
         for gg in range(2):
             regroup(nc.scalar.copy, w2g[:, gg, :, :], w2r[:, gg, :, :])
         nc.vector.tensor_copy(out=b1f[:], in_=b1t[:])
         quant_w1(0, 1)
-        for u in range(4):
+        for u in range(2):
             l1_pass(u, 1)
+        l1(2)
+        l1(3)
         copy_p(1)
         quant_p(1)
         l1(4)

@@ -110,8 +110,8 @@ def tile_mlpconv2d_pa_kernel(tc, x, w1, b1, w2, b2, out):
 
         def regroup(eng_copy, dst, src):
             eng_copy(
-                out=dst.rearrange("p (c i) t -> p c t i", i=4),
-                in_=src.rearrange("p t (c i) -> p c t i", i=4),
+                out=dst.rearrange("p (c i) t -> p c t i", i=8),
+                in_=src.rearrange("p t (c i) -> p c t i", i=8),
             )
 
         def regroup_w1(g, a):

@@ -60,7 +60,7 @@ def tile_mlpconv2d_pa_kernel(tc, x, w1, b1, w2, b2, out):
         res = [keep.tile([P, 2, 2, 256], F32, name="res%d" % t) for t in range(4)]
 
         xf = x.rearrange("n c h w -> n c (h w)")
-        w1v = w1.rearrange("(c a q t) f -> q a c t f", c=16, a=2, q=8, t=4)
+        w1v = w1.rearrange("(c a r) f -> a c r f", c=16, a=2)
         outv = out.rearrange("n (h uh m par) f -> (n h) par m uh f", h=2, uh=2, m=P, par=2)
         outw = out.rearrange("n (h uh m par) f -> (n h) m uh (par f)", h=2, uh=2, m=P, par=2)
 
@@ -68,10 +68,8 @@ def tile_mlpconv2d_pa_kernel(tc, x, w1, b1, w2, b2, out):
             off = 70 * (q // 2) + 4 * (q % 2)
             eng.dma_start(out=dst[q:P:8, 0 : hi - lo], in_=xf[n, :, off + lo : off + hi])
 
-        def load_w1(g, a, first_queue):
-            for q in QORDER:
-                eng = first_queue if q < 4 else nc.sync
-                eng.dma_start(out=w1r[g][a][q:P:8, :, :], in_=w1v[q, a, :, :, 512 * g : 512 * g + 512])
+        def load_w1(eng, g, a):
+            eng.dma_start(out=w1r[g][a][:].rearrange("p t f -> p (t f)"), in_=w1v[a, :, :, 512 * g : 512 * g + 512])
 
         ctx.enter_context(tc.manual_schedule())
         nc.vector.memset(b2z[:], 0.0)
@@ -83,13 +81,13 @@ def tile_mlpconv2d_pa_kernel(tc, x, w1, b1, w2, b2, out):
         for q in QORDER:
             load_x(nc.scalar if q < 4 else nc.sync, xa, 0, q, 0, XHALF)
         nc.scalar.activation(out=warm[:], in_=ones[:, 0:1], func=RELU)
-        load_w1(0, 0, nc.scalar)
-        load_w1(0, 1, nc.sync)
+        load_w1(nc.sync, 0, 0)
+        load_w1(nc.sync, 0, 1)
         nc.sync.dma_start(out=w2r[:], in_=w2.rearrange("(g p t) n -> p g t n", g=2, t=4))
         for q in QORDER:
             load_x(nc.sync, xb, 0, q, 18 * 140, XLEN)
-        load_w1(1, 0, nc.sync)
-        load_w1(1, 1, nc.sync)
+        load_w1(nc.sync, 1, 0)
+        load_w1(nc.sync, 1, 1)
         for q in QORDER:
             load_x(nc.sync, x1, 1, q, 0, XLEN)
 

@@ -17,7 +17,7 @@ P = 128
 ROWS = 34
 XHALF = 2448
 XLEN = 4686
-ACT_SLABS = {(0, 0): 2, (0, 1): 2, (1, 0): 2, (1, 1): 0}
+ACT_SLABS = {(0, 0): 2, (0, 1): 2, (1, 0): 0, (1, 1): 0}
 W2_SLOT = 8
 R_AGE = 7
 QORDER = (0, 4, 1, 5, 2, 6, 3, 7)
@@ -60,16 +60,16 @@ def tile_mlpconv2d_pa_kernel(tc, x, w1, b1, w2, b2, out):
         res = [keep.tile([P, 2, 2, 256], F32, name="res%d" % t) for t in range(4)]
 
         xf = x.rearrange("n c h w -> n c (h w)")
-        w1v = w1.rearrange("(c a r) f -> a c r f", c=16, a=2)
+        w1v = w1.rearrange("(c a i r) f -> a i c r f", c=16, a=2, i=4)
         outv = out.rearrange("n (h uh m par) f -> (n h) par m uh f", h=2, uh=2, m=P, par=2)
         outw = out.rearrange("n (h uh m par) f -> (n h) m uh (par f)", h=2, uh=2, m=P, par=2)
 
         def load_x(eng, dst, n, q, lo, hi):
-            off = 70 * (q // 2) + 4 * (q % 2)
+            off = 70 * (q % 4) + 4 * (q // 4)
             eng.dma_start(out=dst[q:P:8, 0 : hi - lo], in_=xf[n, :, off + lo : off + hi])
 
-        def load_w1(eng, g, a):
-            eng.dma_start(out=w1r[g][a][:].rearrange("p t f -> p (t f)"), in_=w1v[a, :, :, 512 * g : 512 * g + 512])
+        def load_w1(eng, g, a, i):
+            eng.dma_start(out=w1r[g][a][i:P:4, :, :].rearrange("p t f -> p (t f)"), in_=w1v[a, i, :, :, 512 * g : 512 * g + 512])
 
         ctx.enter_context(tc.manual_schedule())
         nc.vector.memset(b2z[:], 0.0)
@@ -81,13 +81,15 @@ def tile_mlpconv2d_pa_kernel(tc, x, w1, b1, w2, b2, out):
         for q in QORDER:
             load_x(nc.scalar if q < 4 else nc.sync, xa, 0, q, 0, XHALF)
         nc.scalar.activation(out=warm[:], in_=ones[:, 0:1], func=RELU)
-        load_w1(nc.sync, 0, 0)
-        load_w1(nc.sync, 0, 1)
-        nc.sync.dma_start(out=w2r[:], in_=w2.rearrange("(g p t) n -> p g t n", g=2, t=4))
+        for a in range(2):
+            for i in range(4):
+                load_w1(nc.sync, 0, a, i)
         for q in QORDER:
             load_x(nc.sync, xb, 0, q, 18 * 140, XLEN)
-        load_w1(nc.sync, 1, 0)
-        load_w1(nc.sync, 1, 1)
+        for a in range(2):
+            for i in range(4):
+                load_w1(nc.sync, 1, a, i)
+        nc.sync.dma_start(out=w2r[:], in_=w2.rearrange("(g p t) n -> p g t n", g=2, t=4))
         for q in QORDER:
             load_x(nc.sync, x1, 1, q, 0, XLEN)
 
@@ -119,11 +121,11 @@ def tile_mlpconv2d_pa_kernel(tc, x, w1, b1, w2, b2, out):
             for tp in range(nv, 4):
                 nc.scalar.copy(out=w1g[:, g, a, tp, :, :], in_=src[:, tp, :, :])
 
-        def quant_w1(g, a):
+        def quant_w1(g, a, lo=0, hi=4):
             nc.vector.quantize_mx(
-                out=w1c[:, g, a, :].bitcast(FP8X4),
-                scales=w1s[:, g, a, :],
-                in_=w1g[:, g, a, :, :, :].rearrange("p tp m t -> p (tp m t)"),
+                out=w1c[:, g, a, P * lo : P * hi].bitcast(FP8X4),
+                scales=w1s[:, g, a, P * lo : P * hi],
+                in_=w1g[:, g, a, lo:hi, :, :].rearrange("p tp m t -> p (tp m t)"),
             )
 
         units = [(t, 4 * g + k) for g in range(2) for t in range(2) for k in range(4)]
@@ -237,33 +239,35 @@ def tile_mlpconv2d_pa_kernel(tc, x, w1, b1, w2, b2, out):
                 return units[s - age][0], units[s - age][1] // 4
             return None, None
 
+        nc.gpsimd.tensor_copy(out=b1f[:], in_=b1t[:])
         copy_p(0)
-        quant_p(0)
         regroup_w1(0, 0)
-        quant_w1(0, 0)
+        quant_p(0)
+        quant_w1(0, 0, 0, 2)
         for u in range(2):
             l1_pass(u, 0)
         regroup_w1(0, 1)
-        for gg in range(2):
-            regroup(nc.scalar.copy, w2g[:, gg, :, :], w2r[:, gg, :, :])
-        nc.vector.tensor_copy(out=b1f[:], in_=b1t[:])
-        quant_w1(0, 1)
+        quant_w1(0, 0, 2, 4)
+        quant_w1(0, 1, 0, 2)
         for u in range(2):
             l1_pass(u, 1)
+        quant_w1(0, 1, 2, 4)
         l1(2)
         l1(3)
         copy_p(1)
         quant_p(1)
+        regroup_w1(1, 0)
         l1(4)
         l1(5)
         b2ps = psum.tile([P, 512], F32, name="b2ps", tag="bank")
         nc.tensor.matmul(out=b2ps[:, 0:256], lhsT=ones[:], rhs=b2z[:], start=True, stop=True)
+        regroup_w1(1, 1)
+        quant_w1(1, 0)
+        quant_w1(1, 1)
         prep = {
-            0: [lambda: regroup_w1(1, 0)],
-            1: [lambda: regroup_w1(1, 1), lambda: quant_w1(1, 0)],
-            2: [lambda: quant_w1(1, 1)],
-            8: [lambda: copy_p(2)],
-            9: [lambda: quant_p(2)],
+            4: [lambda: regroup(nc.scalar.copy, w2g[:, 0, :, :], w2r[:, 0, :, :])],
+            6: [lambda: regroup(nc.scalar.copy, w2g[:, 1, :, :], w2r[:, 1, :, :]), lambda: copy_p(2)],
+            7: [lambda: quant_p(2)],
             16: [lambda: copy_p(3)],
             17: [lambda: quant_p(3)],
         }

@@ -32,9 +32,8 @@ def tile_mlpconv2d_pa_kernel(tc, x, w1, b1, w2, b2, out):
 
         xa = keep.tile([P, 18 * 140], BF16, name="xa", align_bytes=64)
         xb = keep.tile([P, 16 * 140], BF16, name="xb", align_bytes=64)
-        x1 = keep.tile([P, ROWS * 140], BF16, name="x1", align_bytes=64)
-        xsrc = ((xa, 0), (xb, 0), (x1, 0), (x1, 18))
-        grp = [keep.tile([P, ROWS * 128], BF16, name="grp%d" % n, align_bytes=64) for n in range(2)]
+        xsrc = (xa, xb)
+        grp = [keep.tile([P, (18, 16)[t % 2], 2, 64], BF16, name="grp%d" % t, align_bytes=64) for t in range(4)]
         qc = [keep.tile([P, ROWS * 32], U32, name="qc%d" % n, align_bytes=64) for n in range(2)]
         qs = [keep.tile([P, ROWS * 32], U8, name="qs%d" % n, align_bytes=64) for n in range(2)]
         w1r = [
@@ -60,6 +59,7 @@ def tile_mlpconv2d_pa_kernel(tc, x, w1, b1, w2, b2, out):
         res = [keep.tile([P, 2, 2, 256], F32, name="res%d" % t) for t in range(4)]
 
         xf = x.rearrange("n c h w -> n c (h w)")
+        xrow = x.rearrange("n c (m two) w -> n two c m w", two=2)
         w1v = w1.rearrange("(c a i r) f -> a i c r f", c=16, a=2, i=4)
         outv = out.rearrange("n (h uh m par) f -> (n h) par m uh f", h=2, uh=2, m=P, par=2)
         outw = out.rearrange("n (h uh m par) f -> (n h) m uh (par f)", h=2, uh=2, m=P, par=2)
@@ -67,6 +67,12 @@ def tile_mlpconv2d_pa_kernel(tc, x, w1, b1, w2, b2, out):
         def load_x(eng, dst, n, q, lo, hi):
             off = 70 * (q % 4) + 4 * (q // 4)
             eng.dma_start(out=dst[q:P:8, 0 : hi - lo], in_=xf[n, :, off + lo : off + hi])
+
+        def load_rows(eng, t, q, par):
+            i, j = q % 4, q // 4
+            m0, m1 = (0, 18, 34)[t % 2] + i // 2, (18, 34)[t % 2] + i // 2
+            c0 = 4 * j + 2 * par
+            eng.dma_start(out=grp[t][q:P:8, :, par, :], in_=xrow[1, i % 2, :, m0:m1, c0 : c0 + 64])
 
         def load_w1(eng, g, a, i):
             eng.dma_start(out=w1r[g][a][i:P:4, :, :].rearrange("p t f -> p (t f)"), in_=w1v[a, i, :, :, 512 * g : 512 * g + 512])
@@ -90,22 +96,25 @@ def tile_mlpconv2d_pa_kernel(tc, x, w1, b1, w2, b2, out):
             for i in range(4):
                 load_w1(nc.sync, 1, a, i)
         nc.sync.dma_start(out=w2r[:], in_=w2.rearrange("(g p t) n -> p g t n", g=2, t=4))
-        for q in QORDER:
-            load_x(nc.sync, x1, 1, q, 0, XLEN)
+        for t in (2, 3):
+            for q in QORDER:
+                for par in range(2):
+                    load_rows(nc.sync, t, q, par)
 
         def copy_p(t):
-            n, r0, r1 = t // 2, 18 * (t % 2), 18 + 16 * (t % 2)
-            src, s0 = xsrc[t]
-            x32 = src[:].bitcast(F32).rearrange("p (u w) -> p u w", w=70)
-            g32 = grp[n][:].bitcast(F32).rearrange("p (u par w) -> p u par w", par=2, w=32)
+            x32 = xsrc[t][:].bitcast(F32).rearrange("p (u w) -> p u w", w=70)
+            g32 = grp[t][:].bitcast(F32)
             for par in range(2):
-                nc.vector.tensor_copy(out=g32[:, r0:r1, par, :], in_=x32[:, s0 : s0 + r1 - r0, par : par + 32])
+                nc.vector.tensor_copy(out=g32[:, :, par, :], in_=x32[:, :, par : par + 32])
 
         def quant_p(t):
-            n = t // 2
-            for c0, c1 in ((0, 512), (512, 576)) if t % 2 == 0 else ((576, 1088),):
+            n, base = t // 2, 576 * (t % 2)
+            flat = grp[t][:].rearrange("p u par w -> p (u par w)")
+            for c0, c1 in ((0, 512), (512, 576)) if t % 2 == 0 else ((0, 512),):
                 nc.vector.quantize_mx(
-                    out=qc[n][:, c0:c1].bitcast(FP8X4), scales=qs[n][:, c0:c1], in_=grp[n][:, 4 * c0 : 4 * c1]
+                    out=qc[n][:, base + c0 : base + c1].bitcast(FP8X4),
+                    scales=qs[n][:, base + c0 : base + c1],
+                    in_=flat[:, 4 * c0 : 4 * c1],
                 )
 
         def regroup(eng_copy, dst, src):
@@ -240,6 +249,8 @@ def tile_mlpconv2d_pa_kernel(tc, x, w1, b1, w2, b2, out):
             return None, None
 
         nc.gpsimd.tensor_copy(out=b1f[:], in_=b1t[:])
+        b2ps = psum.tile([P, 512], F32, name="b2ps", tag="bank")
+        nc.tensor.matmul(out=b2ps[:, 0:256], lhsT=ones[:], rhs=b2z[:], start=True, stop=True)
         copy_p(0)
         regroup_w1(0, 0)
         quant_p(0)
@@ -252,6 +263,7 @@ def tile_mlpconv2d_pa_kernel(tc, x, w1, b1, w2, b2, out):
         for u in range(2):
             l1_pass(u, 1)
         quant_w1(0, 1, 2, 4)
+        nc.scalar.copy(out=b2bc[:], in_=b2ps[:, 0:256])
         l1(2)
         l1(3)
         copy_p(1)
@@ -259,22 +271,17 @@ def tile_mlpconv2d_pa_kernel(tc, x, w1, b1, w2, b2, out):
         regroup_w1(1, 0)
         l1(4)
         l1(5)
-        b2ps = psum.tile([P, 512], F32, name="b2ps", tag="bank")
-        nc.tensor.matmul(out=b2ps[:, 0:256], lhsT=ones[:], rhs=b2z[:], start=True, stop=True)
         regroup_w1(1, 1)
         quant_w1(1, 0)
         quant_w1(1, 1)
         prep = {
             4: [lambda: regroup(nc.scalar.copy, w2g[:, 0, :, :], w2r[:, 0, :, :])],
-            6: [lambda: regroup(nc.scalar.copy, w2g[:, 1, :, :], w2r[:, 1, :, :]), lambda: copy_p(2)],
+            6: [lambda: regroup(nc.scalar.copy, w2g[:, 1, :, :], w2r[:, 1, :, :])],
             7: [lambda: quant_p(2)],
-            16: [lambda: copy_p(3)],
             17: [lambda: quant_p(3)],
         }
         for s in range(32):
             evac(s)
-            if s == 5:
-                nc.vector.tensor_copy(out=b2bc[:], in_=b2ps[:, 0:256])
             for f in prep.get(s, []):
                 f()
             if s + LEAD < 32:

@@ -19,8 +19,9 @@ XHALF = 2448
 XLEN = 4686
 ACT_SLABS = {(0, 0): 2, (0, 1): 2, (1, 0): 0, (1, 1): 0}
 W2_SLOT = 8
-R_AGE = 7
+R_AGE = 8
 QORDER = (0, 4, 1, 5, 2, 6, 3, 7)
+ACT_HALVES = ((1, 1),)
 LEAD = 6
 
 
@@ -61,7 +62,6 @@ def tile_mlpconv2d_pa_kernel(tc, x, w1, b1, w2, b2, out):
         xf = x.rearrange("n c h w -> n c (h w)")
         xrow = x.rearrange("n c (m two) w -> n two c m w", two=2)
         w1v = w1.rearrange("(c a i r) f -> a i c r f", c=16, a=2, i=4)
-        outv = out.rearrange("n (h uh m par) f -> (n h) par m uh f", h=2, uh=2, m=P, par=2)
         outw = out.rearrange("n (h uh m par) f -> (n h) m uh (par f)", h=2, uh=2, m=P, par=2)
 
         def load_x(eng, dst, n, q, lo, hi):
@@ -127,7 +127,10 @@ def tile_mlpconv2d_pa_kernel(tc, x, w1, b1, w2, b2, out):
             src = w1r[g][a][:].rearrange("p t (m tp) -> p tp m t", tp=4)
             nv = 4 - ACT_SLABS[(g, a)]
             nc.vector.tensor_copy(out=w1g[:, g, a, 0:nv, :, :], in_=src[:, 0:nv, :, :])
-            for tp in range(nv, 4):
+
+        def regroup_w1_act(g, a):
+            src = w1r[g][a][:].rearrange("p t (m tp) -> p tp m t", tp=4)
+            for tp in range(4 - ACT_SLABS[(g, a)], 4):
                 nc.scalar.copy(out=w1g[:, g, a, tp, :, :], in_=src[:, tp, :, :])
 
         def quant_w1(g, a, lo=0, hi=4):
@@ -138,8 +141,27 @@ def tile_mlpconv2d_pa_kernel(tc, x, w1, b1, w2, b2, out):
             )
 
         units = [(t, 4 * g + k) for g in range(2) for t in range(2) for k in range(4)]
-        units += [(t, ft) for t in (2, 3) for ft in range(8)]
+        units += [(2, ft) for ft in range(8)]
+        units += [(3, 4 * uh + j) for uh in range(2) for j in range(4)]
         banks = {}
+
+        def l1_pair(u):
+            uh, j = divmod(units[u][1], 4)
+            banks[u] = psum.tile([P, 512], F32, name="l1_%d" % u, tag="bank")
+            for i in range(2):
+                ft = 2 * j + i
+                g, c0 = ft // 4, P * (ft % 4)
+                for a in range(2):
+                    r0 = 512 + 64 * a + 256 * uh
+                    nc.tensor.matmul_mx(
+                        out=banks[u][:, 256 * i : 256 * i + 256],
+                        lhsT=w1c[:, g, a, c0 : c0 + P].bitcast(FP8X4),
+                        lhsT_scale=w1s[:, g, a, c0 : c0 + P],
+                        rhs=qc[1][:, r0 : r0 + 256].bitcast(FP8X4),
+                        rhs_scale=qs[1][:, r0 : r0 + 256],
+                        start=(a == 0),
+                        stop=(a == 1),
+                    )
 
         def l1_pass(u, a):
             t, ft = units[u]
@@ -158,11 +180,29 @@ def tile_mlpconv2d_pa_kernel(tc, x, w1, b1, w2, b2, out):
             )
 
         def l1(u):
+            if units[u][0] == 3:
+                l1_pair(u)
+                return
             l1_pass(u, 0)
             l1_pass(u, 1)
 
+        def evac_pair(u):
+            uh, j = divmod(units[u][1], 4)
+            for i in range(2):
+                ft = 2 * j + i
+                nc.scalar.activation(
+                    out=hpl[3][:, ft, 256 * uh : 256 * uh + 256].rearrange("p (par u vh) -> p par u vh", u=8, par=2),
+                    in_=banks[u][:, 256 * i : 256 * i + 256].rearrange("p (u par vh) -> p par u vh", u=8, par=2),
+                    func=RELU,
+                    bias=b1f[:, ft : ft + 1],
+                    scale=1.0,
+                )
+
         def evac(u):
             t, ft = units[u]
+            if t == 3:
+                evac_pair(u)
+                return
             nc.scalar.activation(
                 out=hpl[t][:, ft, :].rearrange("p (par u vh) -> p par u vh", u=16, par=2),
                 in_=banks[u][:].rearrange("p (u par vh) -> p par u vh", u=16, par=2),
@@ -201,62 +241,58 @@ def tile_mlpconv2d_pa_kernel(tc, x, w1, b1, w2, b2, out):
 
         last = {}
 
-        def l2_block(b, g):
+        def l2_last(par, g):
             if g == 0:
-                last[b] = psum.tile([P, 512], F32, name="last%d" % b, tag="bank")
+                last[par] = psum.tile([P, 512], F32, name="last%d" % par, tag="bank")
+            c0 = 256 + P * par
             nc.tensor.matmul_mx(
-                out=last[b][:, 0:256],
-                lhsT=hc[3][:, g, P * b : P * b + P].bitcast(FP8X4),
-                lhsT_scale=hs[3][:, g, P * b : P * b + P],
+                out=last[par][:, 0:256],
+                lhsT=hc[3][:, g, c0 : c0 + P].bitcast(FP8X4),
+                lhsT_scale=hs[3][:, g, c0 : c0 + P],
                 rhs=w2c[:, g, :].bitcast(FP8X4),
                 rhs_scale=w2s[:, g, :],
                 start=(g == 0),
                 stop=(g == 1),
             )
 
-        def add_block(b):
-            nc.vector.tensor_tensor(out=res[3][:, b % 2, b // 2, :], in0=last[b][:, 0:256], in1=b2bc[:], op=ADD)
-
-        def relu_block(b, on_vector=False):
-            r = res[3][:, b % 2, b // 2, :]
-            if on_vector:
-                nc.vector.tensor_scalar(out=r, in0=r, scalar1=0.0, scalar2=None, op0=MAX)
-            else:
-                nc.scalar.activation(out=r, in_=r, func=RELU)
+        def add_last(par):
+            nc.vector.tensor_tensor(out=res[3][:, 1, par, :], in0=last[par][:, 0:256], in1=b2bc[:], op=ADD)
 
         def add_b2(t, k):
             nc.vector.tensor_tensor(
-                out=res[t][:, :, k, :],
+                out=res[t][:, k, :, :] if t == 3 else res[t][:, :, k, :],
                 in0=accs[(t, k)][:],
                 in1=b2bc[:].unsqueeze(1).to_broadcast([P, 2, 256]),
                 op=ADD,
             )
 
-        def relu_store(t, k, on_vector=False, halves=False):
+        def relu_store(t, k):
             r = res[t][:, :, k, :]
-            if on_vector:
-                nc.vector.tensor_scalar(out=r, in0=r, scalar1=0.0, scalar2=None, op0=MAX)
-            else:
-                nc.scalar.activation(out=r, in_=r, func=RELU)
-            if halves:
-                nc.sync.dma_start(out=outv[t, k], in_=r)
-            elif k == 1:
+            nc.scalar.activation(out=r, in_=r, func=RELU)
+            if k == 1:
                 nc.sync.dma_start(out=outw[t], in_=res[t][:].rearrange("p uh par f -> p uh (par f)"))
 
         def half_done(s, age):
-            if 0 <= s - age < 31 and units[s - age][1] % 4 == 3:
+            if 0 <= s - age < 24 and units[s - age][1] % 4 == 3:
                 return units[s - age][0], units[s - age][1] // 4
+            return None, None
+
+        def last_done(s, age):
+            if 24 <= s - age < 31 and units[s - age][1] % 2 == 1:
+                return units[s - age][1] // 4, units[s - age][1] % 4 // 2
             return None, None
 
         nc.gpsimd.tensor_copy(out=b1f[:], in_=b1t[:])
         b2ps = psum.tile([P, 512], F32, name="b2ps", tag="bank")
         nc.tensor.matmul(out=b2ps[:, 0:256], lhsT=ones[:], rhs=b2z[:], start=True, stop=True)
         copy_p(0)
+        regroup_w1_act(0, 0)
         regroup_w1(0, 0)
         quant_p(0)
         quant_w1(0, 0, 0, 2)
         for u in range(2):
             l1_pass(u, 0)
+        regroup_w1_act(0, 1)
         regroup_w1(0, 1)
         quant_w1(0, 0, 2, 4)
         quant_w1(0, 1, 0, 2)
@@ -275,9 +311,9 @@ def tile_mlpconv2d_pa_kernel(tc, x, w1, b1, w2, b2, out):
         quant_w1(1, 0)
         quant_w1(1, 1)
         prep = {
-            4: [lambda: regroup(nc.scalar.copy, w2g[:, 0, :, :], w2r[:, 0, :, :])],
-            6: [lambda: regroup(nc.scalar.copy, w2g[:, 1, :, :], w2r[:, 1, :, :])],
-            7: [lambda: quant_p(2)],
+            6: [lambda: regroup(nc.scalar.copy, w2g[:, 0, :, :], w2r[:, 0, :, :])],
+            8: [lambda: regroup(nc.scalar.copy, w2g[:, 1, :, :], w2r[:, 1, :, :])],
+            9: [lambda: quant_p(2)],
             17: [lambda: quant_p(3)],
         }
         for s in range(32):
@@ -289,7 +325,7 @@ def tile_mlpconv2d_pa_kernel(tc, x, w1, b1, w2, b2, out):
             t, g = half_done(s, 0)
             if g is not None:
                 regroup_h(t, g, 0, 256)
-                regroup_h(t, g, 256, 512)
+                regroup_h(t, g, 256, 512, nc.scalar.copy if (t, g) in ACT_HALVES else None)
             if s == W2_SLOT + 2:
                 nc.vector.quantize_mx(
                     out=w2c[:].rearrange("p g n -> p (g n)").bitcast(FP8X4),
@@ -300,34 +336,45 @@ def tile_mlpconv2d_pa_kernel(tc, x, w1, b1, w2, b2, out):
             if g is not None:
                 quant_h(t, g, 0, 256)
                 quant_h(t, g, 256, 512)
-                if g == 1:
-                    l2(t, 0)
-                    l2(t, 1)
-                elif t == 3:
-                    for b in range(4):
-                        l2_block(b, 0)
+            t, g = half_done(s, 1)
+            if g == 1:
+                l2(t, 0)
+                l2(t, 1)
+            uh, g = last_done(s, 0)
+            if g is not None:
+                regroup_h(3, g, 256 * uh, 256 * uh + 256)
+            uh, g = last_done(s, 1)
+            if g is not None:
+                quant_h(3, g, 256 * uh, 256 * uh + 256)
+                if uh == 0 and g == 1:
+                    l2(3, 0)
+                elif uh == 1:
+                    for par in range(2):
+                        l2_last(par, 0)
+            if last_done(s, 3) == (0, 1):
+                add_b2(3, 0)
             for k in range(2):
-                t, g = half_done(s, 3 + k)
+                t, g = half_done(s, 4 + k)
                 if g == 1:
                     add_b2(t, k)
                 t, g = half_done(s, R_AGE + k)
-                if g == 1:
+                if g == 1 and t < 2:
                     relu_store(t, k)
 
-        for b in range(4):
-            regroup_h(3, 1, P * b, P * b + P, nc.vector.tensor_copy if b % 2 == 0 else nc.scalar.copy)
-        for b in range(3):
-            quant_h(3, 1, P * b, P * b + P)
-            l2_block(b, 1)
-        add_block(0)
-        quant_h(3, 1, 3 * P, 4 * P)
-        l2_block(3, 1)
-        add_block(1)
-        relu_block(0)
-        relu_block(1)
-        nc.sync.dma_start(out=outv[3, 0], in_=res[3][:, :, 0, :])
-        add_block(2)
-        add_block(3)
-        relu_block(2)
-        relu_block(3, on_vector=True)
-        nc.sync.dma_start(out=outv[3, 1], in_=res[3][:, :, 1, :])
+        relu_store(2, 0)
+        regroup_h(3, 1, 256, 384, nc.scalar.copy)
+        regroup_h(3, 1, 384, 512, nc.scalar.copy)
+        quant_h(3, 1, 256, 384)
+        l2_last(0, 1)
+        quant_h(3, 1, 384, 512)
+        l2_last(1, 1)
+        relu_store(2, 1)
+        r = res[3][:, 0, :, :]
+        nc.scalar.activation(out=r, in_=r, func=RELU)
+        nc.sync.dma_start(out=outw[3][:, 0, :], in_=r.rearrange("p par f -> p (par f)"))
+        add_last(0)
+        add_last(1)
+        r0, r1 = res[3][:, 1, 0, :], res[3][:, 1, 1, :]
+        nc.scalar.activation(out=r0, in_=r0, func=RELU)
+        nc.vector.tensor_scalar(out=r1, in0=r1, scalar1=0.0, scalar2=None, op0=MAX)
+        nc.sync.dma_start(out=outw[3][:, 1, :], in_=res[3][:, 1, :, :].rearrange("p par f -> p (par f)"))

@@ -21,7 +21,6 @@ ACT_SLABS = {(0, 0): 2, (0, 1): 2, (1, 0): 0, (1, 1): 0}
 W2_SLOT = 8
 R_AGE = 8
 QORDER = (0, 4, 1, 5, 2, 6, 3, 7)
-ACT_HALVES = ((1, 1),)
 LEAD = 6
 
 
@@ -325,7 +324,7 @@ def tile_mlpconv2d_pa_kernel(tc, x, w1, b1, w2, b2, out):
             t, g = half_done(s, 0)
             if g is not None:
                 regroup_h(t, g, 0, 256)
-                regroup_h(t, g, 256, 512, nc.scalar.copy if (t, g) in ACT_HALVES else None)
+                regroup_h(t, g, 256, 512)
             if s == W2_SLOT + 2:
                 nc.vector.quantize_mx(
                     out=w2c[:].rearrange("p g n -> p (g n)").bitcast(FP8X4),
@@ -362,7 +361,7 @@ def tile_mlpconv2d_pa_kernel(tc, x, w1, b1, w2, b2, out):
                     relu_store(t, k)
 
         relu_store(2, 0)
-        regroup_h(3, 1, 256, 384, nc.scalar.copy)
+        regroup_h(3, 1, 256, 384, nc.vector.tensor_copy)
         regroup_h(3, 1, 384, 512, nc.scalar.copy)
         quant_h(3, 1, 256, 384)
         l2_last(0, 1)

@@ -32,7 +32,8 @@ def tile_mlpconv2d_pa_kernel(tc, x, w1, b1, w2, b2, out):
 
         xa = keep.tile([P, 18 * 140], BF16, name="xa", align_bytes=64)
         xb = keep.tile([P, 16 * 140], BF16, name="xb", align_bytes=64)
-        xsrc = (xa, xb)
+        xc = keep.tile([P, 18 * 140], BF16, name="xc", align_bytes=64)
+        xsrc = (xa, xb, xc)
         grp = [keep.tile([P, (18, 16)[t % 2], 2, 64], BF16, name="grp%d" % t, align_bytes=64) for t in range(4)]
         qc = [keep.tile([P, ROWS * 32], U32, name="qc%d" % n, align_bytes=64) for n in range(2)]
         qs = [keep.tile([P, ROWS * 32], U8, name="qs%d" % n, align_bytes=64) for n in range(2)]
@@ -95,10 +96,11 @@ def tile_mlpconv2d_pa_kernel(tc, x, w1, b1, w2, b2, out):
             for i in range(4):
                 load_w1(nc.sync, 1, a, i)
         nc.sync.dma_start(out=w2r[:], in_=w2.rearrange("(g p t) n -> p g t n", g=2, t=4))
-        for t in (2, 3):
-            for q in QORDER:
-                for par in range(2):
-                    load_rows(nc.sync, t, q, par)
+        for q in QORDER:
+            load_x(nc.sync, xc, 1, q, 0, XHALF)
+        for q in QORDER:
+            for par in range(2):
+                load_rows(nc.sync, 3, q, par)
 
         def copy_p(t):
             x32 = xsrc[t][:].bitcast(F32).rearrange("p (u w) -> p u w", w=70)
@@ -310,9 +312,10 @@ def tile_mlpconv2d_pa_kernel(tc, x, w1, b1, w2, b2, out):
         quant_w1(1, 0)
         quant_w1(1, 1)
         prep = {
+            7: [lambda: copy_p(2)],
+            9: [lambda: quant_p(2)],
             6: [lambda: regroup(nc.scalar.copy, w2g[:, 0, :, :], w2r[:, 0, :, :])],
             8: [lambda: regroup(nc.scalar.copy, w2g[:, 1, :, :], w2r[:, 1, :, :])],
-            9: [lambda: quant_p(2)],
             17: [lambda: quant_p(3)],
         }
         for s in range(32):

@@ -47,9 +47,8 @@ def tile_mlpconv2d_pa_kernel(tc, x, w1, b1, w2, b2, out):
         w2g = keep.tile([P, 2, 256, 4], BF16, name="w2g", align_bytes=64)
         w2c = keep.tile([P, 2, 256], U32, name="w2c", align_bytes=64)
         w2s = keep.tile([P, 2, 256], U8, name="w2s", align_bytes=64)
-        b1t = keep.tile([P, 8], BF16, name="b1t")
         b1f = keep.tile([P, 8], F32, name="b1f")
-        b2z = keep.tile([P, 256], BF16, name="b2z")
+        bz = keep.tile([P, 1280], BF16, name="bz")
         ones = keep.tile([P, P], BF16, name="ones")
         b2bc = keep.tile([P, 256], F32, name="b2bc")
         warm = keep.tile([P, 1], BF16, name="warm")
@@ -78,12 +77,10 @@ def tile_mlpconv2d_pa_kernel(tc, x, w1, b1, w2, b2, out):
             eng.dma_start(out=w1r[g][a][i:P:4, :, :].rearrange("p t f -> p (t f)"), in_=w1v[a, i, :, :, 512 * g : 512 * g + 512])
 
         ctx.enter_context(tc.manual_schedule())
-        nc.vector.memset(b2z[:], 0.0)
+        nc.vector.memset(bz[:], 0.0)
         nc.vector.memset(ones[:], 1.0)
-        nc.gpsimd.dma_start(out=b2z[0:1, :], in_=b2.rearrange("(o n) -> o n", o=1))
-        nc.gpsimd.dma_start(
-            out=b1t[:].rearrange("p (g t) -> p g t", g=2), in_=b1.rearrange("(g p t) -> p g t", g=2, t=4)
-        )
+        nc.gpsimd.dma_start(out=bz[0:1, 0:1024], in_=b1.rearrange("(o n) -> o n", o=1))
+        nc.gpsimd.dma_start(out=bz[0:1, 1024:1280], in_=b2.rearrange("(o n) -> o n", o=1))
         for q in QORDER:
             load_x(nc.scalar if q < 4 else nc.sync, xa, 0, q, 0, XHALF)
         nc.scalar.activation(out=warm[:], in_=ones[:, 0:1], func=RELU)
@@ -283,9 +280,13 @@ def tile_mlpconv2d_pa_kernel(tc, x, w1, b1, w2, b2, out):
                 return units[s - age][1] // 4, units[s - age][1] % 4 // 2
             return None, None
 
-        nc.gpsimd.tensor_copy(out=b1f[:], in_=b1t[:])
-        b2ps = psum.tile([P, 512], F32, name="b2ps", tag="bank")
-        nc.tensor.matmul(out=b2ps[:, 0:256], lhsT=ones[:], rhs=b2z[:], start=True, stop=True)
+        bps = psum.tile([P, 512], F32, name="bps", tag="bank")
+        nc.tensor.matmul(out=bps[:, 0:256], lhsT=ones[:], rhs=bz[:, 1024:1280], start=True, stop=True)
+        for ft in range(8):
+            first = 512 * (ft // 4) + ft % 4
+            nc.tensor.matmul(
+                out=bps[:, 256 + ft : 257 + ft], lhsT=bz[:, first : first + 509 : 4], rhs=ones[:, 0:1], start=True, stop=True
+            )
         copy_p(0)
         regroup_w1_act(0, 0)
         regroup_w1(0, 0)
@@ -300,7 +301,8 @@ def tile_mlpconv2d_pa_kernel(tc, x, w1, b1, w2, b2, out):
         for u in range(2):
             l1_pass(u, 1)
         quant_w1(0, 1, 2, 4)
-        nc.scalar.copy(out=b2bc[:], in_=b2ps[:, 0:256])
+        nc.scalar.copy(out=b1f[:], in_=bps[:, 256:264])
+        nc.scalar.copy(out=b2bc[:], in_=bps[:, 0:256])
         l1(2)
         l1(3)
         copy_p(1)

@@ -288,9 +288,9 @@ def tile_mlpconv2d_pa_kernel(tc, x, w1, b1, w2, b2, out):
                 out=bps[:, 256 + ft : 257 + ft], lhsT=bz[:, first : first + 509 : 4], rhs=ones[:, 0:1], start=True, stop=True
             )
         copy_p(0)
+        quant_p(0)
         regroup_w1_act(0, 0)
         regroup_w1(0, 0)
-        quant_p(0)
         quant_w1(0, 0, 0, 2)
         for u in range(2):
             l1_pass(u, 0)
@@ -347,6 +347,8 @@ def tile_mlpconv2d_pa_kernel(tc, x, w1, b1, w2, b2, out):
             uh, g = last_done(s, 0)
             if g is not None:
                 regroup_h(3, g, 256 * uh, 256 * uh + 256)
+            if last_done(s, 3) == (0, 1):
+                add_b2(3, 0)
             uh, g = last_done(s, 1)
             if g is not None:
                 quant_h(3, g, 256 * uh, 256 * uh + 256)
@@ -355,8 +357,6 @@ def tile_mlpconv2d_pa_kernel(tc, x, w1, b1, w2, b2, out):
                 elif uh == 1:
                     for par in range(2):
                         l2_last(par, 0)
-            if last_done(s, 3) == (0, 1):
-                add_b2(3, 0)
             for k in range(2):
                 t, g = half_done(s, 4 + k)
                 if g == 1:

from contextlib import ExitStack

import concourse.mybir as mybir

F32 = mybir.dt.float32
BF16 = mybir.dt.bfloat16
U32 = mybir.dt.uint32
U8 = mybir.dt.uint8
FP8X4 = mybir.dt.float8_e4m3fn_x4
RELU = mybir.ActivationFunctionType.Relu
ADD = mybir.AluOpType.add
MAX = mybir.AluOpType.max

FLOPS = 2 * 2048 * 1024 * 1024 + 2 * 2048 * 1024 * 256

P = 128
ROWS = 34
XHALF = 2448
XLEN = 4686
ACT_SLABS = {(0, 0): 2, (0, 1): 2, (1, 0): 0, (1, 1): 0}
W2_SLOT = 8
R_AGE = 8
QORDER = (0, 4, 1, 5, 2, 6, 3, 7)
LEAD = 6


def tile_mlpconv2d_pa_kernel(tc, x, w1, b1, w2, b2, out):
    nc = tc.nc
    with ExitStack() as ctx:
        keep = ctx.enter_context(tc.tile_pool(name="keep", bufs=1))
        psum = ctx.enter_context(tc.psum_pool(name="psum", bufs=8))

        xa = keep.tile([P, 18 * 140], BF16, name="xa", align_bytes=64)
        xb = keep.tile([P, 16 * 140], BF16, name="xb", align_bytes=64)
        xc = keep.tile([P, 18 * 140], BF16, name="xc", align_bytes=64)
        xsrc = (xa, xb, xc)
        grp = [keep.tile([P, (18, 16)[t % 2], 2, 64], BF16, name="grp%d" % t, align_bytes=64) for t in range(4)]
        qc = [keep.tile([P, ROWS * 32], U32, name="qc%d" % n, align_bytes=64) for n in range(2)]
        qs = [keep.tile([P, ROWS * 32], U8, name="qs%d" % n, align_bytes=64) for n in range(2)]
        w1r = [
            [keep.tile([P, 4, 512], BF16, name="w1r%d%d" % (g, a), align_bytes=64) for a in range(2)] for g in range(2)
        ]
        w1g = keep.tile([P, 2, 2, 4, P, 4], BF16, name="w1g", align_bytes=64)
        w1c = keep.tile([P, 2, 2, 512], U32, name="w1c", align_bytes=64)
        w1s = keep.tile([P, 2, 2, 512], U8, name="w1s", align_bytes=64)
        w2r = keep.tile([P, 2, 4, 256], BF16, name="w2r", align_bytes=64)
        w2g = keep.tile([P, 2, 256, 4], BF16, name="w2g", align_bytes=64)
        w2c = keep.tile([P, 2, 256], U32, name="w2c", align_bytes=64)
        w2s = keep.tile([P, 2, 256], U8, name="w2s", align_bytes=64)
        b1f = keep.tile([P, 8], F32, name="b1f")
        bz = keep.tile([P, 1280], BF16, name="bz")
        ones = keep.tile([P, P], BF16, name="ones")
        b2bc = keep.tile([P, 256], F32, name="b2bc")
        warm = keep.tile([P, 1], BF16, name="warm")
        hpl = [keep.tile([P, 8, 512], BF16, name="hpl%d" % t, align_bytes=64) for t in range(4)]
        hgr = [keep.tile([P, 2, 512, 4], BF16, name="hgr%d" % t, align_bytes=64) for t in range(4)]
        hc = [keep.tile([P, 2, 512], U32, name="hc%d" % t, align_bytes=64) for t in range(4)]
        hs = [keep.tile([P, 2, 512], U8, name="hs%d" % t, align_bytes=64) for t in range(4)]
        res = [keep.tile([P, 2, 2, 256], F32, name="res%d" % t) for t in range(4)]

        xf = x.rearrange("n c h w -> n c (h w)")
        xrow = x.rearrange("n c (m two) w -> n two c m w", two=2)
        w1v = w1.rearrange("(c a i r) f -> a i c r f", c=16, a=2, i=4)
        outw = out.rearrange("n (h uh m par) f -> (n h) m uh (par f)", h=2, uh=2, m=P, par=2)

        def load_x(eng, dst, n, q, lo, hi):
            off = 70 * (q % 4) + 4 * (q // 4)
            eng.dma_start(out=dst[q:P:8, 0 : hi - lo], in_=xf[n, :, off + lo : off + hi])

        def load_rows(eng, t, q, par):
            i, j = q % 4, q // 4
            m0, m1 = (0, 18, 34)[t % 2] + i // 2, (18, 34)[t % 2] + i // 2
            c0 = 4 * j + 2 * par
            eng.dma_start(out=grp[t][q:P:8, :, par, :], in_=xrow[1, i % 2, :, m0:m1, c0 : c0 + 64])

        def load_w1(eng, g, a, i):
            eng.dma_start(out=w1r[g][a][i:P:4, :, :].rearrange("p t f -> p (t f)"), in_=w1v[a, i, :, :, 512 * g : 512 * g + 512])

        ctx.enter_context(tc.manual_schedule())
        nc.vector.memset(bz[:], 0.0)
        nc.vector.memset(ones[:], 1.0)
        nc.gpsimd.dma_start(out=bz[0:1, 0:1024], in_=b1.rearrange("(o n) -> o n", o=1))
        nc.gpsimd.dma_start(out=bz[0:1, 1024:1280], in_=b2.rearrange("(o n) -> o n", o=1))
        for q in QORDER:
            load_x(nc.scalar if q < 4 else nc.sync, xa, 0, q, 0, XHALF)
        nc.scalar.activation(out=warm[:], in_=ones[:, 0:1], func=RELU)
        for a in range(2):
            for i in range(4):
                load_w1(nc.sync, 0, a, i)
        for q in QORDER:
            load_x(nc.sync, xb, 0, q, 18 * 140, XLEN)
        for a in range(2):
            for i in range(4):
                load_w1(nc.sync, 1, a, i)
        nc.sync.dma_start(out=w2r[:], in_=w2.rearrange("(g p t) n -> p g t n", g=2, t=4))
        for q in QORDER:
            load_x(nc.sync, xc, 1, q, 0, XHALF)
        for q in QORDER:
            for par in range(2):
                load_rows(nc.sync, 3, q, par)

        def copy_p(t):
            x32 = xsrc[t][:].bitcast(F32).rearrange("p (u w) -> p u w", w=70)
            g32 = grp[t][:].bitcast(F32)
            for par in range(2):
                nc.vector.tensor_copy(out=g32[:, :, par, :], in_=x32[:, :, par : par + 32])

        def quant_p(t):
            n, base = t // 2, 576 * (t % 2)
            flat = grp[t][:].rearrange("p u par w -> p (u par w)")
            for c0, c1 in ((0, 512), (512, 576)) if t % 2 == 0 else ((0, 512),):
                nc.vector.quantize_mx(
                    out=qc[n][:, base + c0 : base + c1].bitcast(FP8X4),
                    scales=qs[n][:, base + c0 : base + c1],
                    in_=flat[:, 4 * c0 : 4 * c1],
                )

        def regroup(eng_copy, dst, src):
            eng_copy(
                out=dst.rearrange("p (c i) t -> p c t i", i=8),
                in_=src.rearrange("p t (c i) -> p c t i", i=8),
            )

        def regroup_w1(g, a):
            src = w1r[g][a][:].rearrange("p t (m tp) -> p tp m t", tp=4)
            nv = 4 - ACT_SLABS[(g, a)]
            nc.vector.tensor_copy(out=w1g[:, g, a, 0:nv, :, :], in_=src[:, 0:nv, :, :])

        def regroup_w1_act(g, a):
            src = w1r[g][a][:].rearrange("p t (m tp) -> p tp m t", tp=4)
            for tp in range(4 - ACT_SLABS[(g, a)], 4):
                nc.scalar.copy(out=w1g[:, g, a, tp, :, :], in_=src[:, tp, :, :])

        def quant_w1(g, a, lo=0, hi=4):
            nc.vector.quantize_mx(
                out=w1c[:, g, a, P * lo : P * hi].bitcast(FP8X4),
                scales=w1s[:, g, a, P * lo : P * hi],
                in_=w1g[:, g, a, lo:hi, :, :].rearrange("p tp m t -> p (tp m t)"),
            )

        units = [(t, 4 * g + k) for g in range(2) for t in range(2) for k in range(4)]
        units += [(2, ft) for ft in range(8)]
        units += [(3, 4 * uh + j) for uh in range(2) for j in range(4)]
        banks = {}

        def l1_pair(u):
            uh, j = divmod(units[u][1], 4)
            banks[u] = psum.tile([P, 512], F32, name="l1_%d" % u, tag="bank")
            for i in range(2):
                ft = 2 * j + i
                g, c0 = ft // 4, P * (ft % 4)
                for a in range(2):
                    r0 = 512 + 64 * a + 256 * uh
                    nc.tensor.matmul_mx(
                        out=banks[u][:, 256 * i : 256 * i + 256],
                        lhsT=w1c[:, g, a, c0 : c0 + P].bitcast(FP8X4),
                        lhsT_scale=w1s[:, g, a, c0 : c0 + P],
                        rhs=qc[1][:, r0 : r0 + 256].bitcast(FP8X4),
                        rhs_scale=qs[1][:, r0 : r0 + 256],
                        start=(a == 0),
                        stop=(a == 1),
                    )

        def l1_pass(u, a):
            t, ft = units[u]
            if a == 0:
                banks[u] = psum.tile([P, 512], F32, name="l1_%d" % u, tag="bank")
            g, c0 = ft // 4, P * (ft % 4)
            r0 = 512 * (t % 2) + 64 * a
            nc.tensor.matmul_mx(
                out=banks[u][:],
                lhsT=w1c[:, g, a, c0 : c0 + P].bitcast(FP8X4),
                lhsT_scale=w1s[:, g, a, c0 : c0 + P],
                rhs=qc[t // 2][:, r0 : r0 + 512].bitcast(FP8X4),
                rhs_scale=qs[t // 2][:, r0 : r0 + 512],
                start=(a == 0),
                stop=(a == 1),
            )

        def l1(u):
            if units[u][0] == 3:
                l1_pair(u)
                return
            l1_pass(u, 0)
            l1_pass(u, 1)

        def evac_pair(u):
            uh, j = divmod(units[u][1], 4)
            for i in range(2):
                ft = 2 * j + i
                nc.scalar.activation(
                    out=hpl[3][:, ft, 256 * uh : 256 * uh + 256].rearrange("p (par u vh) -> p par u vh", u=8, par=2),
                    in_=banks[u][:, 256 * i : 256 * i + 256].rearrange("p (u par vh) -> p par u vh", u=8, par=2),
                    func=RELU,
                    bias=b1f[:, ft : ft + 1],
                    scale=1.0,
                )

        def evac(u):
            t, ft = units[u]
            if t == 3:
                evac_pair(u)
                return
            nc.scalar.activation(
                out=hpl[t][:, ft, :].rearrange("p (par u vh) -> p par u vh", u=16, par=2),
                in_=banks[u][:].rearrange("p (u par vh) -> p par u vh", u=16, par=2),
                func=RELU,
                bias=b1f[:, ft : ft + 1],
                scale=1.0,
            )

        def regroup_h(t, g, c0=0, c1=512, eng_copy=None):
            regroup(eng_copy or nc.vector.tensor_copy, hgr[t][:, g, c0:c1, :], hpl[t][:, 4 * g : 4 * g + 4, c0:c1])

        def quant_h(t, g, c0=0, c1=512):
            nc.vector.quantize_mx(
                out=hc[t][:, g, c0:c1].bitcast(FP8X4),
                scales=hs[t][:, g, c0:c1],
                in_=hgr[t][:, g, c0:c1, :].rearrange("p c t -> p (c t)"),
            )

        accs = {}

        def l2(t, k):
            acc = psum.tile([P, 2, 256], F32, name="acc%d_%d" % (t, k), tag="bank")
            accs[(t, k)] = acc
            for s in range(2):
                c0 = P * (2 * k + s)
                for g in range(2):
                    nc.tensor.matmul_mx(
                        out=acc[:, s, :],
                        lhsT=hc[t][:, g, c0 : c0 + P].bitcast(FP8X4),
                        lhsT_scale=hs[t][:, g, c0 : c0 + P],
                        rhs=w2c[:, g, :].bitcast(FP8X4),
                        rhs_scale=w2s[:, g, :],
                        start=(g == 0),
                        stop=(g == 1),
                    )

        last = {}

        def l2_last(par, g):
            if g == 0:
                last[par] = psum.tile([P, 512], F32, name="last%d" % par, tag="bank")
            c0 = 256 + P * par
            nc.tensor.matmul_mx(
                out=last[par][:, 0:256],
                lhsT=hc[3][:, g, c0 : c0 + P].bitcast(FP8X4),
                lhsT_scale=hs[3][:, g, c0 : c0 + P],
                rhs=w2c[:, g, :].bitcast(FP8X4),
                rhs_scale=w2s[:, g, :],
                start=(g == 0),
                stop=(g == 1),
            )

        def add_last(par):
            nc.vector.tensor_tensor(out=res[3][:, 1, par, :], in0=last[par][:, 0:256], in1=b2bc[:], op=ADD)

        def add_b2(t, k):
            nc.vector.tensor_tensor(
                out=res[t][:, k, :, :] if t == 3 else res[t][:, :, k, :],
                in0=accs[(t, k)][:],
                in1=b2bc[:].unsqueeze(1).to_broadcast([P, 2, 256]),
                op=ADD,
            )

        def relu_store(t, k):
            r = res[t][:, :, k, :]
            nc.scalar.activation(out=r, in_=r, func=RELU)
            if k == 1:
                nc.sync.dma_start(out=outw[t], in_=res[t][:].rearrange("p uh par f -> p uh (par f)"))

        def half_done(s, age):
            if 0 <= s - age < 24 and units[s - age][1] % 4 == 3:
                return units[s - age][0], units[s - age][1] // 4
            return None, None

        def last_done(s, age):
            if 24 <= s - age < 31 and units[s - age][1] % 2 == 1:
                return units[s - age][1] // 4, units[s - age][1] % 4 // 2
            return None, None

        bps = psum.tile([P, 512], F32, name="bps", tag="bank")
        nc.tensor.matmul(out=bps[:, 0:256], lhsT=ones[:], rhs=bz[:, 1024:1280], start=True, stop=True)
        for ft in range(8):
            first = 512 * (ft // 4) + ft % 4
            nc.tensor.matmul(
                out=bps[:, 256 + ft : 257 + ft], lhsT=bz[:, first : first + 509 : 4], rhs=ones[:, 0:1], start=True, stop=True
            )
        copy_p(0)
        quant_p(0)
        regroup_w1_act(0, 0)
        regroup_w1(0, 0)
        quant_w1(0, 0, 0, 2)
        for u in range(2):
            l1_pass(u, 0)
        regroup_w1_act(0, 1)
        regroup_w1(0, 1)
        quant_w1(0, 0, 2, 4)
        quant_w1(0, 1, 0, 2)
        for u in range(2):
            l1_pass(u, 1)
        quant_w1(0, 1, 2, 4)
        nc.scalar.copy(out=b1f[:], in_=bps[:, 256:264])
        nc.scalar.copy(out=b2bc[:], in_=bps[:, 0:256])
        l1(2)
        l1(3)
        copy_p(1)
        quant_p(1)
        regroup_w1(1, 0)
        l1(4)
        l1(5)
        regroup_w1(1, 1)
        quant_w1(1, 0)
        quant_w1(1, 1)
        prep = {
            7: [lambda: copy_p(2)],
            9: [lambda: quant_p(2)],
            6: [lambda: regroup(nc.scalar.copy, w2g[:, 0, :, :], w2r[:, 0, :, :])],
            8: [lambda: regroup(nc.scalar.copy, w2g[:, 1, :, :], w2r[:, 1, :, :])],
            17: [lambda: quant_p(3)],
        }
        for s in range(32):
            evac(s)
            for f in prep.get(s, []):
                f()
            if s + LEAD < 32:
                l1(s + LEAD)
            t, g = half_done(s, 0)
            if g is not None:
                regroup_h(t, g, 0, 256)
                regroup_h(t, g, 256, 512)
            if s == W2_SLOT + 2:
                nc.vector.quantize_mx(
                    out=w2c[:].rearrange("p g n -> p (g n)").bitcast(FP8X4),
                    scales=w2s[:].rearrange("p g n -> p (g n)"),
                    in_=w2g[:].rearrange("p g n t -> p (g n t)"),
                )
            t, g = half_done(s, 1)
            if g is not None:
                quant_h(t, g, 0, 256)
                quant_h(t, g, 256, 512)
            t, g = half_done(s, 1)
            if g == 1:
                l2(t, 0)
                l2(t, 1)
            uh, g = last_done(s, 0)
            if g is not None:
                regroup_h(3, g, 256 * uh, 256 * uh + 256)
            if last_done(s, 3) == (0, 1):
                add_b2(3, 0)
            uh, g = last_done(s, 1)
            if g is not None:
                quant_h(3, g, 256 * uh, 256 * uh + 256)
                if uh == 0 and g == 1:
                    l2(3, 0)
                elif uh == 1:
                    for par in range(2):
                        l2_last(par, 0)
            for k in range(2):
                t, g = half_done(s, 4 + k)
                if g == 1:
                    add_b2(t, k)
                t, g = half_done(s, R_AGE + k)
                if g == 1 and t < 2:
                    relu_store(t, k)

        relu_store(2, 0)
        regroup_h(3, 1, 256, 384, nc.vector.tensor_copy)
        regroup_h(3, 1, 384, 512, nc.scalar.copy)
        quant_h(3, 1, 256, 384)
        l2_last(0, 1)
        quant_h(3, 1, 384, 512)
        l2_last(1, 1)
        relu_store(2, 1)
        r = res[3][:, 0, :, :]
        nc.scalar.activation(out=r, in_=r, func=RELU)
        nc.sync.dma_start(out=outw[3][:, 0, :], in_=r.rearrange("p par f -> p (par f)"))
        add_last(0)
        add_last(1)
        r0, r1 = res[3][:, 1, 0, :], res[3][:, 1, 1, :]
        nc.scalar.activation(out=r0, in_=r0, func=RELU)
        nc.vector.tensor_scalar(out=r1, in0=r1, scalar1=0.0, scalar2=None, op0=MAX)
        nc.sync.dma_start(out=outw[3][:, 1, :], in_=res[3][:, 1, :, :].rearrange("p par f -> p (par f)"))
